import numpy as np
import ml_dtypes


def mxq(x, axis, fmt="e4m3"):
    dtype, down = {"e4m3": (ml_dtypes.float8_e4m3fn, 7), "e5m2": (ml_dtypes.float8_e5m2, 14)}[fmt]
    v = np.moveaxis(np.asarray(x, np.float32).astype(ml_dtypes.bfloat16).astype(np.float64), axis, -1)
    blocks = v.reshape(v.shape[:-1] + (-1, 32))
    amax = np.abs(blocks).max(-1, keepdims=True)
    byte = np.maximum(np.where(amax > 0, np.frexp(amax)[1] - 1 + 127, 0) - down, 1)
    scale = np.exp2(byte - 127.0)
    codes = (blocks / scale).astype(np.float32).astype(dtype).astype(np.float64)
    return np.moveaxis((codes * scale).reshape(v.shape), -1, axis)


WIDE = False


def mx_kscale(k):
    if not WIDE:
        return np.ones(k)
    levels = np.array([10, -10, 5, -5, 0])
    a = np.random.permutation(np.resize(levels, k // 512 * 4)).reshape(k // 512, 4)
    idx = np.arange(k)
    return np.exp2(a[idx // 512, idx % 128 // 32])


BF16 = ml_dtypes.bfloat16


def bf(x):
    return np.asarray(x, np.float32).astype(BF16)


def f64(x):
    return np.asarray(x).astype(np.float64)


B, HI, WI, F, D, NH, C = 1, 64, 64, 1024, 256, 3, 16
N = HI * WI
EPS = 1e-12


def l2norm_rows(a):
    n = np.sqrt(np.sum(a * a, axis=1, keepdims=True))
    return a / np.maximum(n, EPS)


def setup_inputs():
    s = mx_kscale(F)

    def w():
        return bf(np.random.standard_normal((D, F)) / np.sqrt(F) / s[None, :])

    def b():
        return bf(np.random.standard_normal(D) * 0.2)

    return {"x": bf(np.random.standard_normal((B, F, HI, WI)) * s[None, :, None, None]),
            "W1": w(), "b1": b(), "W2": w(), "b2": b(), "W3": w(), "b3": b()}


def reference(x, W1, b1, W2, b2, W3, b3):
    xq = mxq(f64(x).reshape(F, N).T, 1, "e4m3")
    heads = [l2norm_rows((xq @ mxq(f64(W), 1, "e4m3").T) + f64(b)) for W, b in ((W1, b1), (W2, b2), (W3, b3))]
    return np.stack(heads)

@@ -1,0 +1,234 @@
+from contextlib import ExitStack
+
+import concourse.mybir as mybir
+from concourse.masks import make_identity
+
+F32 = mybir.dt.float32
+BF16 = mybir.dt.bfloat16
+U32 = mybir.dt.uint32
+U8 = mybir.dt.uint8
+FP8X4 = mybir.dt.float8_e4m3fn_x4
+ACT = mybir.ActivationFunctionType
+ALU = mybir.AluOpType
+
+P = 128
+PACK = 4
+K_PASS = P * PACK
+FEATURES = 1024
+PASSES = FEATURES // K_PASS
+NODES = 4096
+HEADS = 3
+DIM = 256
+EPS = 1e-12
+
+CHUNK = 512
+CHUNKS = NODES // CHUNK
+PAIR = 2
+STEP = PAIR * P
+STEPS = NODES // STEP
+STEPS_PER_CHUNK = CHUNK // STEP
+RUN = 4
+
+FLOPS = 2 * NODES * FEATURES * HEADS * DIM
+
+
+def tile_gat_pa_t_kernel(tc, x, W1, b1, W2, b2, W3, b3, out):
+    nc = tc.nc
+    x_rows = x.rearrange("b f i j -> (b f) (i j)")
+
+    with ExitStack() as stack:
+        const = stack.enter_context(tc.tile_pool(name="const", bufs=1))
+        resident = stack.enter_context(tc.tile_pool(name="resident", bufs=CHUNKS))
+        prep = stack.enter_context(tc.tile_pool(name="prep", bufs=3))
+        stage = stack.enter_context(tc.tile_pool(name="stage", bufs=3))
+        quantised = stack.enter_context(tc.tile_pool(name="quantised", bufs=4))
+        biased = stack.enter_context(tc.tile_pool(name="biased", bufs=4))
+        scratch = stack.enter_context(tc.tile_pool(name="scratch", bufs=2))
+        results = stack.enter_context(tc.tile_pool(name="results", bufs=3))
+        small = stack.enter_context(tc.tile_pool(name="small", bufs=4))
+        psum_prep = stack.enter_context(tc.psum_pool(name="psum_prep", bufs=2))
+        psum = stack.enter_context(tc.psum_pool(name="psum", bufs=2 * HEADS))
+
+        identity = const.tile([P, P], F32)
+        make_identity(nc, identity[:])
+        ones = const.tile([P, P], BF16)
+        nc.vector.memset(ones[:], 1.0)
+        bias_rows = const.tile([P, HEADS, DIM], BF16)
+        nc.vector.memset(bias_rows[:], 0.0)
+        one = const.tile([P, 1], F32)
+        nc.vector.memset(one[:], 1.0)
+        nc.scalar.activation(out=one[:], in_=one[:], func=ACT.Sqrt)
+
+        for k, b in enumerate((b1, b2, b3)):
+            nc.scalar.dma_start(out=bias_rows[0:1, k, :], in_=b.rearrange("(o d) -> o d", o=1))
+        w_rows = const.tile([P, HEADS, DIM // P, FEATURES], BF16)
+        x_raw = []
+        for c in range(CHUNKS):
+            if c == 1:
+                for k, w in enumerate((W1, W2, W3)):
+                    nc.sync.dma_start(out=w_rows[:, k], in_=w.rearrange("(half p) f -> p half f", p=P))
+            raw = resident.tile([P, PASSES, PACK, CHUNK], BF16)
+            for g in range(PASSES):
+                nc.sync.dma_start(
+                    out=raw[:, g],
+                    in_=x_rows[g * K_PASS : (g + 1) * K_PASS, c * CHUNK : (c + 1) * CHUNK].rearrange(
+                        "(p j) n -> p j n", j=PACK
+                    ),
+                )
+            x_raw.append(raw)
+
+        bias_all = const.tile([P, HEADS, DIM], F32)
+        w_codes = const.tile([P, PASSES, HEADS, DIM], U32, align_bytes=64)
+        w_scales = const.tile([P, PASSES, HEADS, DIM], U8, align_bytes=64)
+
+        def prepare_weights_and_biases():
+            for k in range(HEADS):
+                for g in range(PASSES):
+                    flipped = psum_prep.tile([P, 2, DIM], F32, tag="prep")
+                    for half in range(DIM // P):
+                        words = (
+                            w_rows[:, k, half, :].bitcast(F32).rearrange("d (g p u) -> d g u p", g=PASSES, u=2)
+                        )
+                        for u in range(2):
+                            nc.tensor.transpose(
+                                out=flipped[:, u, half * P : (half + 1) * P],
+                                in_=words[:, g, u, :],
+                                identity=identity[:],
+                            )
+                    w_grouped = prep.tile([P, DIM, 2], F32, align_bytes=64)
+                    nc.scalar.copy(out=w_grouped[:], in_=flipped[:].rearrange("p u d -> p d u"))
+                    nc.vector.quantize_mx(
+                        out=w_codes[:, g, k, :].bitcast(FP8X4),
+                        scales=w_scales[:, g, k, :],
+                        in_=w_grouped[:].rearrange("p d u -> p (d u)").bitcast(BF16),
+                    )
+            for k in range(HEADS):
+                spread = psum_prep.tile([P, DIM], F32, tag="prep")
+                nc.tensor.matmul(out=spread[:], lhsT=ones[:], rhs=bias_rows[:, k, :], start=True, stop=True)
+                nc.vector.tensor_copy(out=bias_all[:, k, :], in_=spread[:])
+
+        grouped, x_codes, x_scales, sums, biased_rows, sumsq, inv_sumsq, inv_norm = {}, {}, {}, {}, {}, {}, {}, {}
+
+        def regroup(s):
+            if not 0 <= s < STEPS:
+                return
+            c, part = divmod(s, STEPS_PER_CHUNK)
+            side_by_side = stage.tile([P, PASSES, STEP, PACK], BF16, align_bytes=64)
+            nc.vector.tensor_copy(
+                out=side_by_side[:].rearrange("p g (c i) j -> p g c j i", i=RUN),
+                in_=x_raw[c][:, :, :, part * STEP : (part + 1) * STEP].rearrange("p g j (c i) -> p g c j i", i=RUN),
+            )
+            grouped[s] = side_by_side
+
+        def quantise(s):
+            if not 0 <= s < STEPS:
+                return
+            codes = quantised.tile([P, PASSES, STEP], U32, align_bytes=64)
+            scales = quantised.tile([P, PASSES, STEP], U8, align_bytes=64)
+            nc.vector.quantize_mx(
+                out=codes[:].rearrange("p g n -> p (g n)").bitcast(FP8X4),
+                scales=scales[:].rearrange("p g n -> p (g n)"),
+                in_=grouped[s][:].rearrange("p g n j -> p (g n j)"),
+            )
+            x_codes[s], x_scales[s] = codes, scales
+
+        def multiply(s):
+            if not 0 <= s < STEPS:
+                return
+            for k in range(HEADS):
+                acc = psum.tile([P, PAIR, DIM], F32)
+                for i in range(PAIR):
+                    nodes = slice(i * P, (i + 1) * P)
+                    for g in range(PASSES):
+                        nc.tensor.matmul_mx(
+                            out=acc[:, i, :],
+                            lhsT=x_codes[s][:, g, nodes].bitcast(FP8X4),
+                            lhsT_scale=x_scales[s][:, g, nodes],
+                            rhs=w_codes[:, g, k, :].bitcast(FP8X4),
+                            rhs_scale=w_scales[:, g, k, :],
+                            start=(g == 0),
+                            stop=(g == PASSES - 1),
+                        )
+                sums[s, k] = acc
+
+        def add_bias(s):
+            if not 0 <= s < STEPS:
+                return
+            h = biased.tile([P, HEADS, PAIR, DIM], F32)
+            for k in range(HEADS):
+                nc.vector.tensor_tensor(
+                    out=h[:, k],
+                    in0=sums[s, k][:],
+                    in1=bias_all[:, k, :].unsqueeze(1).to_broadcast([P, PAIR, DIM]),
+                    op=ALU.add,
+                )
+            biased_rows[s] = h
+
+        def sum_squares(s):
+            if not 0 <= s < STEPS:
+                return
+            squares = scratch.tile([P, HEADS, PAIR, DIM], F32)
+            total = small.tile([P, HEADS, PAIR], F32)
+            for k in range(HEADS):
+                for i in range(PAIR):
+                    nc.scalar.activation(
+                        out=squares[:, k, i, :],
+                        in_=biased_rows[s][:, k, i, :],
+                        func=ACT.Square,
+                        accum_out=total[:, k, i : i + 1],
+                    )
+            sumsq[s] = total
+
+        def invert_sums(s):
+            if not 0 <= s < STEPS:
+                return
+            floored = small.tile([P, HEADS, PAIR], F32)
+            nc.vector.tensor_scalar_max(out=floored[:], in0=sumsq[s][:], scalar1=EPS * EPS)
+            inverse = small.tile([P, HEADS, PAIR], F32)
+            nc.vector.reciprocal(out=inverse[:], in_=floored[:])
+            inv_sumsq[s] = inverse
+
+        def scale_and_store(s):
+            if not 0 <= s < STEPS:
+                return
+            root = small.tile([P, HEADS, PAIR], F32)
+            nc.scalar.activation(out=root[:], in_=inv_sumsq[s][:], func=ACT.Sqrt)
+            inv_norm[s] = root
+            result = results.tile([P, HEADS, PAIR, DIM], F32)
+            for k in range(HEADS):
+                for i in range(PAIR):
+                    if k < HEADS - 1:
+                        nc.scalar.activation(
+                            out=result[:, k, i, :],
+                            in_=biased_rows[s][:, k, i, :],
+                            func=ACT.Copy,
+                            scale=inv_norm[s][:, k, i : i + 1],
+                        )
+                    else:
+                        nc.gpsimd.tensor_scalar(
+                            out=result[:, k, i, :],
+                            in0=biased_rows[s][:, k, i, :],
+                            scalar1=inv_norm[s][:, k, i : i + 1],
+                            scalar2=0.0,
+                            op0=ALU.mult,
+                            op1=ALU.add,
+                        )
+                first_node = s * STEP
+                nc.sync.dma_start(
+                    out=out[k, first_node : first_node + STEP, :].rearrange("(i m) d -> m i d", m=P),
+                    in_=result[:, k],
+                )
+
+        regroup(0)
+        quantise(0)
+        prepare_weights_and_biases()
+        regroup(1)
+        quantise(1)
+        for s in range(STEPS):
+            multiply(s)
+            add_bias(s)
+            sum_squares(s)
+            invert_sums(s)
+            scale_and_store(s)
+            regroup(s + 2)
+            quantise(s + 2)

@@ -197,22 +197,12 @@ def tile_gat_pa_t_kernel(tc, x, W1, b1, W2, b2, W3, b3, out):
             result = results.tile([P, HEADS, PAIR, DIM], F32)
             for k in range(HEADS):
                 for i in range(PAIR):
-                    if k < HEADS - 1:
-                        nc.scalar.activation(
-                            out=result[:, k, i, :],
-                            in_=biased_rows[s][:, k, i, :],
-                            func=ACT.Copy,
-                            scale=inv_norm[s][:, k, i : i + 1],
-                        )
-                    else:
-                        nc.gpsimd.tensor_scalar(
-                            out=result[:, k, i, :],
-                            in0=biased_rows[s][:, k, i, :],
-                            scalar1=inv_norm[s][:, k, i : i + 1],
-                            scalar2=0.0,
-                            op0=ALU.mult,
-                            op1=ALU.add,
-                        )
+                    nc.scalar.activation(
+                        out=result[:, k, i, :],
+                        in_=biased_rows[s][:, k, i, :],
+                        func=ACT.Copy,
+                        scale=inv_norm[s][:, k, i : i + 1],
+                    )
                 first_node = s * STEP
                 nc.sync.dma_start(
                     out=out[k, first_node : first_node + STEP, :].rearrange("(i m) d -> m i d", m=P),

@@ -27,6 +27,8 @@ PAIR = 2
 STEP = PAIR * P
 STEPS = NODES // STEP
 STEPS_PER_CHUNK = CHUNK // STEP
+AHEAD = 2
+SCALAR_REGROUPS_EVERY = 5
 RUN = 4
 
 FLOPS = 2 * NODES * FEATURES * HEADS * DIM
@@ -40,42 +42,52 @@ def tile_gat_pa_t_kernel(tc, x, W1, b1, W2, b2, W3, b3, out):
         const = stack.enter_context(tc.tile_pool(name="const", bufs=1))
         resident = stack.enter_context(tc.tile_pool(name="resident", bufs=CHUNKS))
         prep = stack.enter_context(tc.tile_pool(name="prep", bufs=3))
-        stage = stack.enter_context(tc.tile_pool(name="stage", bufs=3))
+        stage = stack.enter_context(tc.tile_pool(name="stage", bufs=4))
         quantised = stack.enter_context(tc.tile_pool(name="quantised", bufs=4))
         biased = stack.enter_context(tc.tile_pool(name="biased", bufs=4))
         scratch = stack.enter_context(tc.tile_pool(name="scratch", bufs=2))
-        results = stack.enter_context(tc.tile_pool(name="results", bufs=3))
+        results = stack.enter_context(tc.tile_pool(name="results", bufs=4))
         small = stack.enter_context(tc.tile_pool(name="small", bufs=4))
         psum_prep = stack.enter_context(tc.psum_pool(name="psum_prep", bufs=2))
         psum = stack.enter_context(tc.psum_pool(name="psum", bufs=2 * HEADS))
 
         identity = const.tile([P, P], F32)
         make_identity(nc, identity[:])
-        ones = const.tile([P, P], BF16)
-        nc.vector.memset(ones[:], 1.0)
         bias_rows = const.tile([P, HEADS, DIM], BF16)
         nc.vector.memset(bias_rows[:], 0.0)
+        ones = const.tile([P, P], BF16)
+        nc.vector.memset(ones[:], 1.0)
         one = const.tile([P, 1], F32)
         nc.vector.memset(one[:], 1.0)
         nc.scalar.activation(out=one[:], in_=one[:], func=ACT.Sqrt)
 
         for k, b in enumerate((b1, b2, b3)):
-            nc.scalar.dma_start(out=bias_rows[0:1, k, :], in_=b.rearrange("(o d) -> o d", o=1))
+            nc.sync.dma_start(out=bias_rows[0:1, k, :], in_=b.rearrange("(o d) -> o d", o=1))
         w_rows = const.tile([P, HEADS, DIM // P, FEATURES], BF16)
         x_raw = []
         for c in range(CHUNKS):
-            if c == 1:
-                for k, w in enumerate((W1, W2, W3)):
-                    nc.sync.dma_start(out=w_rows[:, k], in_=w.rearrange("(half p) f -> p half f", p=P))
             raw = resident.tile([P, PASSES, PACK, CHUNK], BF16)
+            x_raw.append(raw)
+
+        def load_nodes(c, first, count):
             for g in range(PASSES):
                 nc.sync.dma_start(
-                    out=raw[:, g],
-                    in_=x_rows[g * K_PASS : (g + 1) * K_PASS, c * CHUNK : (c + 1) * CHUNK].rearrange(
-                        "(p j) n -> p j n", j=PACK
-                    ),
+                    out=x_raw[c][:, g, :, first : first + count],
+                    in_=x_rows[
+                        g * K_PASS : (g + 1) * K_PASS, c * CHUNK + first : c * CHUNK + first + count
+                    ].rearrange("(p j) n -> p j n", j=PACK),
                 )
-            x_raw.append(raw)
+
+        def load_weights(k, w):
+            nc.sync.dma_start(out=w_rows[:, k], in_=w.rearrange("(half p) f -> p half f", p=P))
+
+        load_weights(0, W1)
+        load_nodes(0, 0, STEP)
+        load_weights(1, W2)
+        load_weights(2, W3)
+        load_nodes(0, STEP, CHUNK - STEP)
+        for c in range(1, CHUNKS):
+            load_nodes(c, 0, CHUNK)
 
         bias_all = const.tile([P, HEADS, DIM], F32)
         w_codes = const.tile([P, PASSES, HEADS, DIM], U32, align_bytes=64)
@@ -109,15 +121,21 @@ def tile_gat_pa_t_kernel(tc, x, W1, b1, W2, b2, W3, b3, out):
 
         grouped, x_codes, x_scales, sums, biased_rows, sumsq, inv_sumsq, inv_norm = {}, {}, {}, {}, {}, {}, {}, {}
 
+        def scalar_regroups(s):
+            return s % SCALAR_REGROUPS_EVERY == SCALAR_REGROUPS_EVERY - 2
+
         def regroup(s):
             if not 0 <= s < STEPS:
                 return
             c, part = divmod(s, STEPS_PER_CHUNK)
             side_by_side = stage.tile([P, PASSES, STEP, PACK], BF16, align_bytes=64)
-            nc.vector.tensor_copy(
-                out=side_by_side[:].rearrange("p g (c i) j -> p g c j i", i=RUN),
-                in_=x_raw[c][:, :, :, part * STEP : (part + 1) * STEP].rearrange("p g j (c i) -> p g c j i", i=RUN),
-            )
+            target = side_by_side[:].rearrange("p g (c i) j -> p g c j i", i=RUN)
+            source = x_raw[c][:, :, :, part * STEP : (part + 1) * STEP].rearrange("p g j (c i) -> p g c j i", i=RUN)
+            if scalar_regroups(s):
+                for g in range(PASSES):
+                    nc.scalar.copy(out=target[:, g], in_=source[:, g])
+            else:
+                nc.vector.tensor_copy(out=target, in_=source)
             grouped[s] = side_by_side
 
         def quantise(s):
@@ -197,12 +215,28 @@ def tile_gat_pa_t_kernel(tc, x, W1, b1, W2, b2, W3, b3, out):
             result = results.tile([P, HEADS, PAIR, DIM], F32)
             for k in range(HEADS):
                 for i in range(PAIR):
-                    nc.scalar.activation(
-                        out=result[:, k, i, :],
-                        in_=biased_rows[s][:, k, i, :],
-                        func=ACT.Copy,
-                        scale=inv_norm[s][:, k, i : i + 1],
-                    )
+                    if i == 0 and s >= STEPS - AHEAD:
+                        nc.vector.tensor_scalar_mul(
+                            out=result[:, k, i, :],
+                            in0=biased_rows[s][:, k, i, :],
+                            scalar1=inv_norm[s][:, k, i : i + 1],
+                        )
+                    elif i == 0:
+                        nc.scalar.activation(
+                            out=result[:, k, i, :],
+                            in_=biased_rows[s][:, k, i, :],
+                            func=ACT.Copy,
+                            scale=inv_norm[s][:, k, i : i + 1],
+                        )
+                    else:
+                        nc.gpsimd.tensor_scalar(
+                            out=result[:, k, i, :],
+                            in0=biased_rows[s][:, k, i, :],
+                            scalar1=inv_norm[s][:, k, i : i + 1],
+                            scalar2=0.0,
+                            op0=ALU.mult,
+                            op1=ALU.add,
+                        )
                 first_node = s * STEP
                 nc.sync.dma_start(
                     out=out[k, first_node : first_node + STEP, :].rearrange("(i m) d -> m i d", m=P),
@@ -220,5 +254,8 @@ def tile_gat_pa_t_kernel(tc, x, W1, b1, W2, b2, W3, b3, out):
             sum_squares(s)
             invert_sums(s)
             scale_and_store(s)
-            regroup(s + 2)
-            quantise(s + 2)
+            if scalar_regroups(s + AHEAD + 1):
+                regroup(s + AHEAD + 1)
+            if not scalar_regroups(s + AHEAD):
+                regroup(s + AHEAD)
+            quantise(s + AHEAD)

@@ -21,15 +21,16 @@ HEADS = 3
 DIM = 256
 EPS = 1e-12
 
-CHUNK = 512
-CHUNKS = NODES // CHUNK
+GROUP = 512
+GROUPS = NODES // GROUP
+SIDE = GROUP // P
+CHUNK_GROUPS = (1, 1, 2, 2, 2)
 PAIR = 2
 STEP = PAIR * P
 STEPS = NODES // STEP
-STEPS_PER_CHUNK = CHUNK // STEP
+STEPS_PER_GROUP = GROUP // STEP
 AHEAD = 2
 SCALAR_REGROUPS_EVERY = 5
-RUN = 4
 
 FLOPS = 2 * NODES * FEATURES * HEADS * DIM
 
@@ -40,7 +41,6 @@ def tile_gat_pa_t_kernel(tc, x, W1, b1, W2, b2, W3, b3, out):
 
     with ExitStack() as stack:
         const = stack.enter_context(tc.tile_pool(name="const", bufs=1))
-        resident = stack.enter_context(tc.tile_pool(name="resident", bufs=CHUNKS))
         prep = stack.enter_context(tc.tile_pool(name="prep", bufs=3))
         stage = stack.enter_context(tc.tile_pool(name="stage", bufs=4))
         quantised = stack.enter_context(tc.tile_pool(name="quantised", bufs=4))
@@ -65,16 +65,22 @@ def tile_gat_pa_t_kernel(tc, x, W1, b1, W2, b2, W3, b3, out):
             nc.sync.dma_start(out=bias_rows[0:1, k, :], in_=b.rearrange("(o d) -> o d", o=1))
         w_rows = const.tile([P, HEADS, DIM // P, FEATURES], BF16)
         x_raw = []
-        for c in range(CHUNKS):
-            raw = resident.tile([P, PASSES, PACK, CHUNK], BF16)
+        first_node = []
+        home = {}
+        for c, groups in enumerate(CHUNK_GROUPS):
+            raw = const.tile([P, PASSES, PACK, groups * GROUP], BF16, name="x_raw%d" % c)
             x_raw.append(raw)
+            first_node.append(len(home) * GROUP)
+            for part in range(groups):
+                home[len(home)] = (c, part * GROUP)
 
-        def load_nodes(c, first, count):
+        def load_nodes(c):
+            count = CHUNK_GROUPS[c] * GROUP
             for g in range(PASSES):
                 nc.sync.dma_start(
-                    out=x_raw[c][:, g, :, first : first + count],
+                    out=x_raw[c][:, g, :, :],
                     in_=x_rows[
-                        g * K_PASS : (g + 1) * K_PASS, c * CHUNK + first : c * CHUNK + first + count
+                        g * K_PASS : (g + 1) * K_PASS, first_node[c] : first_node[c] + count
                     ].rearrange("(p j) n -> p j n", j=PACK),
                 )
 
@@ -82,12 +88,11 @@ def tile_gat_pa_t_kernel(tc, x, W1, b1, W2, b2, W3, b3, out):
             nc.sync.dma_start(out=w_rows[:, k], in_=w.rearrange("(half p) f -> p half f", p=P))
 
         load_weights(0, W1)
-        load_nodes(0, 0, STEP)
+        load_nodes(0)
         load_weights(1, W2)
         load_weights(2, W3)
-        load_nodes(0, STEP, CHUNK - STEP)
-        for c in range(1, CHUNKS):
-            load_nodes(c, 0, CHUNK)
+        for c in range(1, len(CHUNK_GROUPS)):
+            load_nodes(c)
 
         bias_all = const.tile([P, HEADS, DIM], F32)
         w_codes = const.tile([P, PASSES, HEADS, DIM], U32, align_bytes=64)
@@ -127,10 +132,13 @@ def tile_gat_pa_t_kernel(tc, x, W1, b1, W2, b2, W3, b3, out):
         def regroup(s):
             if not 0 <= s < STEPS:
                 return
-            c, part = divmod(s, STEPS_PER_CHUNK)
+            group, part = divmod(s, STEPS_PER_GROUP)
+            c, first = home[group]
             side_by_side = stage.tile([P, PASSES, STEP, PACK], BF16, align_bytes=64)
-            target = side_by_side[:].rearrange("p g (c i) j -> p g c j i", i=RUN)
-            source = x_raw[c][:, :, :, part * STEP : (part + 1) * STEP].rearrange("p g j (c i) -> p g c j i", i=RUN)
+            target = side_by_side[:].rearrange("p g (i m) j -> p g m j i", i=PAIR)
+            source = x_raw[c][:, :, :, first : first + GROUP].rearrange("p g j (m r) -> p g m j r", r=SIDE)[
+                :, :, :, :, part * PAIR : (part + 1) * PAIR
+            ]
             if scalar_regroups(s):
                 for g in range(PASSES):
                     nc.scalar.copy(out=target[:, g], in_=source[:, g])
@@ -237,9 +245,11 @@ def tile_gat_pa_t_kernel(tc, x, W1, b1, W2, b2, W3, b3, out):
                             op0=ALU.mult,
                             op1=ALU.add,
                         )
-                first_node = s * STEP
+                group, part = divmod(s, STEPS_PER_GROUP)
                 nc.sync.dma_start(
-                    out=out[k, first_node : first_node + STEP, :].rearrange("(i m) d -> m i d", m=P),
+                    out=out[k, group * GROUP : (group + 1) * GROUP, :].rearrange("(m r) d -> m r d", r=SIDE)[
+                        :, part * PAIR : (part + 1) * PAIR, :
+                    ],
                     in_=result[:, k],
                 )
 

@@ -22,15 +22,12 @@ DIM = 256
 EPS = 1e-12
 
 GROUP = 512
-GROUPS = NODES // GROUP
 SIDE = GROUP // P
 CHUNK_GROUPS = (1, 1, 2, 2, 2)
 PAIR = 2
 STEP = PAIR * P
 STEPS = NODES // STEP
 STEPS_PER_GROUP = GROUP // STEP
-AHEAD = 2
-SCALAR_REGROUPS_EVERY = 5
 
 FLOPS = 2 * NODES * FEATURES * HEADS * DIM
 
@@ -44,12 +41,13 @@ def tile_gat_pa_t_kernel(tc, x, W1, b1, W2, b2, W3, b3, out):
         prep = stack.enter_context(tc.tile_pool(name="prep", bufs=3))
         stage = stack.enter_context(tc.tile_pool(name="stage", bufs=4))
         quantised = stack.enter_context(tc.tile_pool(name="quantised", bufs=4))
-        biased = stack.enter_context(tc.tile_pool(name="biased", bufs=4))
+        biased = stack.enter_context(tc.tile_pool(name="biased", bufs=5))
         scratch = stack.enter_context(tc.tile_pool(name="scratch", bufs=2))
-        results = stack.enter_context(tc.tile_pool(name="results", bufs=4))
-        small = stack.enter_context(tc.tile_pool(name="small", bufs=4))
+        results = stack.enter_context(tc.tile_pool(name="results", bufs=5))
+        small = stack.enter_context(tc.tile_pool(name="small", bufs=5))
         psum_prep = stack.enter_context(tc.psum_pool(name="psum_prep", bufs=2))
         psum = stack.enter_context(tc.psum_pool(name="psum", bufs=2 * HEADS))
+        stack.enter_context(tc.manual_schedule())
 
         identity = const.tile([P, P], F32)
         make_identity(nc, identity[:])
@@ -61,8 +59,6 @@ def tile_gat_pa_t_kernel(tc, x, W1, b1, W2, b2, W3, b3, out):
         nc.vector.memset(one[:], 1.0)
         nc.scalar.activation(out=one[:], in_=one[:], func=ACT.Sqrt)
 
-        for k, b in enumerate((b1, b2, b3)):
-            nc.sync.dma_start(out=bias_rows[0:1, k, :], in_=b.rearrange("(o d) -> o d", o=1))
         w_rows = const.tile([P, HEADS, DIM // P, FEATURES], BF16)
         x_raw = []
         first_node = []
@@ -74,77 +70,82 @@ def tile_gat_pa_t_kernel(tc, x, W1, b1, W2, b2, W3, b3, out):
             for part in range(groups):
                 home[len(home)] = (c, part * GROUP)
 
-        def load_nodes(c):
+        def load_nodes(c, g):
             count = CHUNK_GROUPS[c] * GROUP
-            for g in range(PASSES):
-                nc.sync.dma_start(
-                    out=x_raw[c][:, g, :, :],
-                    in_=x_rows[
-                        g * K_PASS : (g + 1) * K_PASS, first_node[c] : first_node[c] + count
-                    ].rearrange("(p j) n -> p j n", j=PACK),
-                )
+            nc.sync.dma_start(
+                out=x_raw[c][:, g, :, :],
+                in_=x_rows[g * K_PASS : (g + 1) * K_PASS, first_node[c] : first_node[c] + count].rearrange(
+                    "(p j) n -> p j n", j=PACK
+                ),
+            )
 
         def load_weights(k, w):
             nc.sync.dma_start(out=w_rows[:, k], in_=w.rearrange("(half p) f -> p half f", p=P))
 
+        load_nodes(0, 0)
         load_weights(0, W1)
-        load_nodes(0)
+        load_nodes(0, 1)
+        for k, b in enumerate((b1, b2, b3)):
+            nc.sync.dma_start(out=bias_rows[0:1, k, :], in_=b.rearrange("(o d) -> o d", o=1))
         load_weights(1, W2)
         load_weights(2, W3)
         for c in range(1, len(CHUNK_GROUPS)):
-            load_nodes(c)
+            for g in range(PASSES):
+                load_nodes(c, g)
 
         bias_all = const.tile([P, HEADS, DIM], F32)
         w_codes = const.tile([P, PASSES, HEADS, DIM], U32, align_bytes=64)
         w_scales = const.tile([P, PASSES, HEADS, DIM], U8, align_bytes=64)
 
-        def prepare_weights_and_biases():
-            for k in range(HEADS):
-                for g in range(PASSES):
-                    flipped = psum_prep.tile([P, 2, DIM], F32, tag="prep")
-                    for half in range(DIM // P):
-                        words = (
-                            w_rows[:, k, half, :].bitcast(F32).rearrange("d (g p u) -> d g u p", g=PASSES, u=2)
+        def prepare_weights(k):
+            for g in range(PASSES):
+                flipped = psum_prep.tile([P, 2, DIM], F32, tag="prep")
+                for half in range(DIM // P):
+                    words = w_rows[:, k, half, :].bitcast(F32).rearrange("d (g p u) -> d g u p", g=PASSES, u=2)
+                    for u in range(2):
+                        nc.tensor.transpose(
+                            out=flipped[:, u, half * P : (half + 1) * P],
+                            in_=words[:, g, u, :],
+                            identity=identity[:],
                         )
-                        for u in range(2):
-                            nc.tensor.transpose(
-                                out=flipped[:, u, half * P : (half + 1) * P],
-                                in_=words[:, g, u, :],
-                                identity=identity[:],
-                            )
-                    w_grouped = prep.tile([P, DIM, 2], F32, align_bytes=64)
-                    nc.scalar.copy(out=w_grouped[:], in_=flipped[:].rearrange("p u d -> p d u"))
-                    nc.vector.quantize_mx(
-                        out=w_codes[:, g, k, :].bitcast(FP8X4),
-                        scales=w_scales[:, g, k, :],
-                        in_=w_grouped[:].rearrange("p d u -> p (d u)").bitcast(BF16),
-                    )
+                w_grouped = prep.tile([P, DIM, 2], F32, align_bytes=64)
+                nc.scalar.copy(out=w_grouped[:], in_=flipped[:].rearrange("p u d -> p d u"))
+                nc.vector.quantize_mx(
+                    out=w_codes[:, g, k, :].bitcast(FP8X4),
+                    scales=w_scales[:, g, k, :],
+                    in_=w_grouped[:].rearrange("p d u -> p (d u)").bitcast(BF16),
+                )
+
+        def spread_biases():
             for k in range(HEADS):
                 spread = psum_prep.tile([P, DIM], F32, tag="prep")
                 nc.tensor.matmul(out=spread[:], lhsT=ones[:], rhs=bias_rows[:, k, :], start=True, stop=True)
                 nc.vector.tensor_copy(out=bias_all[:, k, :], in_=spread[:])
 
-        grouped, x_codes, x_scales, sums, biased_rows, sumsq, inv_sumsq, inv_norm = {}, {}, {}, {}, {}, {}, {}, {}
+        grouped, x_codes, x_scales, sums, biased_rows, sumsq, norm, floored, inv_norm, result = (
+            {}, {}, {}, {}, {}, {}, {}, {}, {}, {},
+        )
 
-        def scalar_regroups(s):
-            return s % SCALAR_REGROUPS_EVERY == SCALAR_REGROUPS_EVERY - 2
-
-        def regroup(s):
+        def regroup_pass(s, g, engine):
             if not 0 <= s < STEPS:
                 return
             group, part = divmod(s, STEPS_PER_GROUP)
             c, first = home[group]
-            side_by_side = stage.tile([P, PASSES, STEP, PACK], BF16, align_bytes=64)
-            target = side_by_side[:].rearrange("p g (i m) j -> p g m j i", i=PAIR)
-            source = x_raw[c][:, :, :, first : first + GROUP].rearrange("p g j (m r) -> p g m j r", r=SIDE)[
-                :, :, :, :, part * PAIR : (part + 1) * PAIR
+            if g == 0:
+                side_by_side = stage.tile([P, PASSES, STEP, PACK], BF16, align_bytes=64)
+                grouped[s] = side_by_side
+            target = grouped[s][:, g].rearrange("p (i m) j -> p m j i", i=PAIR)
+            source = x_raw[c][:, g, :, first : first + GROUP].rearrange("p j (m r) -> p m j r", r=SIDE)[
+                :, :, :, part * PAIR : (part + 1) * PAIR
             ]
-            if scalar_regroups(s):
-                for g in range(PASSES):
-                    nc.scalar.copy(out=target[:, g], in_=source[:, g])
-            else:
+            if engine == "vector":
                 nc.vector.tensor_copy(out=target, in_=source)
-            grouped[s] = side_by_side
+            else:
+                nc.scalar.copy(out=target, in_=source)
+
+        def regroup(s):
+            regroup_pass(s, 0, "vector")
+            regroup_pass(s, 1, "scalar")
 
         def quantise(s):
             if not 0 <= s < STEPS:
@@ -205,67 +206,95 @@ def tile_gat_pa_t_kernel(tc, x, W1, b1, W2, b2, W3, b3, out):
                     )
             sumsq[s] = total
 
-        def invert_sums(s):
-            if not 0 <= s < STEPS:
-                return
-            floored = small.tile([P, HEADS, PAIR], F32)
-            nc.vector.tensor_scalar_max(out=floored[:], in0=sumsq[s][:], scalar1=EPS * EPS)
-            inverse = small.tile([P, HEADS, PAIR], F32)
-            nc.vector.reciprocal(out=inverse[:], in_=floored[:])
-            inv_sumsq[s] = inverse
-
-        def scale_and_store(s):
+        def take_root(s):
             if not 0 <= s < STEPS:
                 return
             root = small.tile([P, HEADS, PAIR], F32)
-            nc.scalar.activation(out=root[:], in_=inv_sumsq[s][:], func=ACT.Sqrt)
-            inv_norm[s] = root
-            result = results.tile([P, HEADS, PAIR, DIM], F32)
-            for k in range(HEADS):
-                for i in range(PAIR):
-                    if i == 0 and s >= STEPS - AHEAD:
-                        nc.vector.tensor_scalar_mul(
-                            out=result[:, k, i, :],
-                            in0=biased_rows[s][:, k, i, :],
-                            scalar1=inv_norm[s][:, k, i : i + 1],
-                        )
-                    elif i == 0:
-                        nc.scalar.activation(
-                            out=result[:, k, i, :],
-                            in_=biased_rows[s][:, k, i, :],
-                            func=ACT.Copy,
-                            scale=inv_norm[s][:, k, i : i + 1],
-                        )
-                    else:
-                        nc.gpsimd.tensor_scalar(
-                            out=result[:, k, i, :],
-                            in0=biased_rows[s][:, k, i, :],
-                            scalar1=inv_norm[s][:, k, i : i + 1],
-                            scalar2=0.0,
-                            op0=ALU.mult,
-                            op1=ALU.add,
-                        )
-                group, part = divmod(s, STEPS_PER_GROUP)
-                nc.sync.dma_start(
-                    out=out[k, group * GROUP : (group + 1) * GROUP, :].rearrange("(m r) d -> m r d", r=SIDE)[
-                        :, part * PAIR : (part + 1) * PAIR, :
-                    ],
-                    in_=result[:, k],
+            nc.scalar.activation(out=root[:], in_=sumsq[s][:], func=ACT.Sqrt)
+            norm[s] = root
+
+        def floor_norm(s):
+            if not 0 <= s < STEPS:
+                return
+            least = small.tile([P, HEADS, PAIR], F32)
+            nc.vector.tensor_scalar_max(out=least[:], in0=norm[s][:], scalar1=EPS)
+            floored[s] = least
+
+        def invert(s):
+            if not 0 <= s < STEPS:
+                return
+            inverse = small.tile([P, HEADS, PAIR], F32)
+            nc.vector.reciprocal(out=inverse[:], in_=floored[s][:])
+            inv_norm[s] = inverse
+            scaled = results.tile([P, HEADS, PAIR, DIM], F32)
+            result[s] = scaled
+
+        def scale(s, k, i, engine):
+            target = result[s][:, k, i, :]
+            rows = biased_rows[s][:, k, i, :]
+            factor = inv_norm[s][:, k, i : i + 1]
+            if engine == "vector":
+                nc.vector.tensor_scalar_mul(out=target, in0=rows, scalar1=factor)
+            elif engine == "scalar":
+                nc.scalar.activation(out=target, in_=rows, func=ACT.Copy, scale=factor)
+            else:
+                nc.gpsimd.tensor_scalar(
+                    out=target, in0=rows, scalar1=factor, scalar2=0.0, op0=ALU.mult, op1=ALU.add
                 )
 
-        regroup(0)
+        def store(s, k):
+            group, part = divmod(s, STEPS_PER_GROUP)
+            nc.sync.dma_start(
+                out=out[k, group * GROUP : (group + 1) * GROUP, :].rearrange("(m r) d -> m r d", r=SIDE)[
+                    :, part * PAIR : (part + 1) * PAIR, :
+                ],
+                in_=result[s][:, k],
+            )
+
+        def second_engine(s):
+            return "gpsimd" if s < STEPS - 2 else "scalar"
+
+        def scale_early(s):
+            if not 0 <= s < STEPS:
+                return
+            if second_engine(s) == "gpsimd":
+                for k in range(HEADS):
+                    scale(s, k, 1, "gpsimd")
+
+        def scale_late(s):
+            if not 0 <= s < STEPS:
+                return
+            for k in range(HEADS):
+                scale(s, k, 0, "vector")
+                if second_engine(s) == "scalar":
+                    scale(s, k, 1, "scalar")
+                store(s, k)
+
+        regroup_pass(0, 0, "vector")
+        regroup_pass(1, 0, "vector")
+        prepare_weights(0)
+        regroup_pass(0, 1, "vector")
+        regroup_pass(1, 1, "scalar")
         quantise(0)
-        prepare_weights_and_biases()
-        regroup(1)
+        prepare_weights(1)
         quantise(1)
-        for s in range(STEPS):
-            multiply(s)
-            add_bias(s)
-            sum_squares(s)
-            invert_sums(s)
-            scale_and_store(s)
-            if scalar_regroups(s + AHEAD + 1):
-                regroup(s + AHEAD + 1)
-            if not scalar_regroups(s + AHEAD):
-                regroup(s + AHEAD)
-            quantise(s + AHEAD)
+        prepare_weights(2)
+        spread_biases()
+        multiply(0)
+        for t in range(STEPS + 2):
+            multiply(t + 1)
+            add_bias(t)
+            sum_squares(t)
+            scale_late(t - 2)
+            floor_norm(t - 1)
+            if t == 0:
+                regroup_pass(2, 0, "vector")
+                regroup_pass(2, 1, "vector")
+                regroup(3)
+                quantise(2)
+            else:
+                quantise(t + 2)
+                regroup(t + 3)
+            take_root(t)
+            invert(t - 1)
+            scale_early(t - 1)

@@ -265,7 +265,7 @@ def tile_gat_pa_t_kernel(tc, x, W1, b1, W2, b2, W3, b3, out):
             if not 0 <= s < STEPS:
                 return
             for k in range(HEADS):
-                scale(s, k, 0, "vector")
+                scale(s, k, 0, "scalar" if k == 0 and second_engine(s) == "gpsimd" else "vector")
                 if second_engine(s) == "scalar":
                     scale(s, k, 1, "scalar")
                 store(s, k)

@@ -294,7 +294,8 @@ def tile_gat_pa_t_kernel(tc, x, W1, b1, W2, b2, W3, b3, out):
                 quantise(2)
             else:
                 quantise(t + 2)
-                regroup(t + 3)
-            take_root(t)
             invert(t - 1)
             scale_early(t - 1)
+            if t > 0:
+                regroup(t + 3)
+            take_root(t)

@@ -29,6 +29,8 @@ STEP = PAIR * P
 STEPS = NODES // STEP
 STEPS_PER_GROUP = GROUP // STEP
 
+SOON = 3
+
 FLOPS = 2 * NODES * FEATURES * HEADS * DIM
 
 
@@ -57,7 +59,7 @@ def tile_gat_pa_t_kernel(tc, x, W1, b1, W2, b2, W3, b3, out):
         nc.vector.memset(ones[:], 1.0)
         one = const.tile([P, 1], F32)
         nc.vector.memset(one[:], 1.0)
-        nc.scalar.activation(out=one[:], in_=one[:], func=ACT.Sqrt)
+        nc.scalar.activation(out=one[:], in_=one[:], func=ACT.Abs_reciprocal_sqrt)
 
         w_rows = const.tile([P, HEADS, DIM // P, FEATURES], BF16)
         x_raw = []
@@ -210,21 +212,19 @@ def tile_gat_pa_t_kernel(tc, x, W1, b1, W2, b2, W3, b3, out):
             if not 0 <= s < STEPS:
                 return
             root = small.tile([P, HEADS, PAIR], F32)
-            nc.scalar.activation(out=root[:], in_=sumsq[s][:], func=ACT.Sqrt)
+            nc.scalar.activation(out=root[:], in_=sumsq[s][:], func=ACT.Abs_reciprocal_sqrt)
             norm[s] = root
 
         def floor_norm(s):
             if not 0 <= s < STEPS:
                 return
-            least = small.tile([P, HEADS, PAIR], F32)
-            nc.vector.tensor_scalar_max(out=least[:], in0=norm[s][:], scalar1=EPS)
-            floored[s] = least
+            return
 
         def invert(s):
             if not 0 <= s < STEPS:
                 return
             inverse = small.tile([P, HEADS, PAIR], F32)
-            nc.vector.reciprocal(out=inverse[:], in_=floored[s][:])
+            nc.vector.tensor_scalar_min(out=inverse[:], in0=norm[s][:], scalar1=1.0 / EPS)
             inv_norm[s] = inverse
             scaled = results.tile([P, HEADS, PAIR, DIM], F32)
             result[s] = scaled
@@ -265,9 +265,11 @@ def tile_gat_pa_t_kernel(tc, x, W1, b1, W2, b2, W3, b3, out):
             if not 0 <= s < STEPS:
                 return
             for k in range(HEADS):
-                scale(s, k, 0, "scalar" if k == 0 and second_engine(s) == "gpsimd" else "vector")
-                if second_engine(s) == "scalar":
-                    scale(s, k, 1, "scalar")
+                if second_engine(s) == "gpsimd":
+                    scale(s, k, 0, "scalar" if k == 0 else "vector")
+                else:
+                    scale(s, k, 0, "vector")
+                    scale(s, k, 1, "scalar" if k >= STEPS - s else "vector")
                 store(s, k)
 
         regroup_pass(0, 0, "vector")
@@ -281,12 +283,12 @@ def tile_gat_pa_t_kernel(tc, x, W1, b1, W2, b2, W3, b3, out):
         prepare_weights(2)
         spread_biases()
         multiply(0)
-        for t in range(STEPS + 2):
+        for t in range(STEPS + 1):
             multiply(t + 1)
             add_bias(t)
             sum_squares(t)
-            scale_late(t - 2)
-            floor_norm(t - 1)
+            if t - 2 < STEPS - SOON:
+                scale_late(t - 2)
             if t == 0:
                 regroup_pass(2, 0, "vector")
                 regroup_pass(2, 1, "vector")
@@ -296,6 +298,8 @@ def tile_gat_pa_t_kernel(tc, x, W1, b1, W2, b2, W3, b3, out):
                 quantise(t + 2)
             invert(t - 1)
             scale_early(t - 1)
+            if t - 1 >= STEPS - SOON:
+                scale_late(t - 1)
             if t > 0:
                 regroup(t + 3)
             take_root(t)

@@ -266,7 +266,7 @@ def tile_gat_pa_t_kernel(tc, x, W1, b1, W2, b2, W3, b3, out):
                 return
             for k in range(HEADS):
                 if second_engine(s) == "gpsimd":
-                    scale(s, k, 0, "scalar" if k == 0 else "vector")
+                    scale(s, k, 0, "scalar" if k == 0 and s % 2 == 0 else "vector")
                 else:
                     scale(s, k, 0, "vector")
                     scale(s, k, 1, "scalar" if k >= STEPS - s else "vector")

@@ -84,13 +84,13 @@ def tile_gat_pa_t_kernel(tc, x, W1, b1, W2, b2, W3, b3, out):
         def load_weights(k, w):
             nc.sync.dma_start(out=w_rows[:, k], in_=w.rearrange("(half p) f -> p half f", p=P))
 
-        load_nodes(0, 0)
         load_weights(0, W1)
-        load_nodes(0, 1)
+        load_weights(1, W2)
         for k, b in enumerate((b1, b2, b3)):
             nc.sync.dma_start(out=bias_rows[0:1, k, :], in_=b.rearrange("(o d) -> o d", o=1))
-        load_weights(1, W2)
+        load_nodes(0, 0)
         load_weights(2, W3)
+        load_nodes(0, 1)
         for c in range(1, len(CHUNK_GROUPS)):
             for g in range(PASSES):
                 load_nodes(c, g)
@@ -99,30 +99,38 @@ def tile_gat_pa_t_kernel(tc, x, W1, b1, W2, b2, W3, b3, out):
         w_codes = const.tile([P, PASSES, HEADS, DIM], U32, align_bytes=64)
         w_scales = const.tile([P, PASSES, HEADS, DIM], U8, align_bytes=64)
 
-        def prepare_weights(k):
-            for g in range(PASSES):
-                flipped = psum_prep.tile([P, 2, DIM], F32, tag="prep")
-                for half in range(DIM // P):
-                    words = w_rows[:, k, half, :].bitcast(F32).rearrange("d (g p u) -> d g u p", g=PASSES, u=2)
-                    for u in range(2):
-                        nc.tensor.transpose(
-                            out=flipped[:, u, half * P : (half + 1) * P],
-                            in_=words[:, g, u, :],
-                            identity=identity[:],
-                        )
-                w_grouped = prep.tile([P, DIM, 2], F32, align_bytes=64)
-                nc.scalar.copy(out=w_grouped[:], in_=flipped[:].rearrange("p u d -> p d u"))
-                nc.vector.quantize_mx(
-                    out=w_codes[:, g, k, :].bitcast(FP8X4),
-                    scales=w_scales[:, g, k, :],
-                    in_=w_grouped[:].rearrange("p d u -> p (d u)").bitcast(BF16),
-                )
+        turned = {}
+
+        def turn_weights(k, g):
+            flipped = psum_prep.tile([P, 2, DIM], F32, tag="prep")
+            for half in range(DIM // P):
+                words = w_rows[:, k, half, :].bitcast(F32).rearrange("d (g p u) -> d g u p", g=PASSES, u=2)
+                for u in range(2):
+                    nc.tensor.transpose(
+                        out=flipped[:, u, half * P : (half + 1) * P],
+                        in_=words[:, g, u, :],
+                        identity=identity[:],
+                    )
+            w_grouped = prep.tile([P, DIM, 2], F32, align_bytes=64)
+            nc.scalar.copy(out=w_grouped[:], in_=flipped[:].rearrange("p u d -> p d u"))
+            turned[k, g] = w_grouped
+
+        def quantise_weights(k, g):
+            nc.vector.quantize_mx(
+                out=w_codes[:, g, k, :].bitcast(FP8X4),
+                scales=w_scales[:, g, k, :],
+                in_=turned[k, g][:].rearrange("p d u -> p (d u)").bitcast(BF16),
+            )
+
+        def prepare_weights(k, g):
+            turn_weights(k, g)
+            quantise_weights(k, g)
 
         def spread_biases():
             for k in range(HEADS):
                 spread = psum_prep.tile([P, DIM], F32, tag="prep")
                 nc.tensor.matmul(out=spread[:], lhsT=ones[:], rhs=bias_rows[:, k, :], start=True, stop=True)
-                nc.vector.tensor_copy(out=bias_all[:, k, :], in_=spread[:])
+                nc.scalar.copy(out=bias_all[:, k, :], in_=spread[:])
 
         grouped, x_codes, x_scales, sums, biased_rows, sumsq, norm, floored, inv_norm, result = (
             {}, {}, {}, {}, {}, {}, {}, {}, {}, {},
@@ -272,16 +280,20 @@ def tile_gat_pa_t_kernel(tc, x, W1, b1, W2, b2, W3, b3, out):
                     scale(s, k, 1, "scalar" if k >= STEPS - s else "vector")
                 store(s, k)
 
+        prepare_weights(0, 0)
+        prepare_weights(0, 1)
+        spread_biases()
         regroup_pass(0, 0, "vector")
         regroup_pass(1, 0, "vector")
-        prepare_weights(0)
+        prepare_weights(1, 0)
+        prepare_weights(1, 1)
         regroup_pass(0, 1, "vector")
+        prepare_weights(2, 0)
         regroup_pass(1, 1, "scalar")
         quantise(0)
-        prepare_weights(1)
+        turn_weights(2, 1)
         quantise(1)
-        prepare_weights(2)
-        spread_biases()
+        quantise_weights(2, 1)
         multiply(0)
         for t in range(STEPS + 1):
             multiply(t + 1)
@@ -299,7 +311,9 @@ def tile_gat_pa_t_kernel(tc, x, W1, b1, W2, b2, W3, b3, out):
             invert(t - 1)
             scale_early(t - 1)
             if t - 1 >= STEPS - SOON:
+                take_root(t)
                 scale_late(t - 1)
-            if t > 0:
-                regroup(t + 3)
-            take_root(t)
+            else:
+                if t > 0:
+                    regroup(t + 3)
+                take_root(t)

@@ -295,6 +295,8 @@ def tile_gat_pa_t_kernel(tc, x, W1, b1, W2, b2, W3, b3, out):
         quantise(1)
         quantise_weights(2, 1)
         multiply(0)
+        regroup_pass(2, 0, "vector")
+        regroup_pass(2, 1, "scalar")
         for t in range(STEPS + 1):
             multiply(t + 1)
             add_bias(t)
@@ -302,8 +304,6 @@ def tile_gat_pa_t_kernel(tc, x, W1, b1, W2, b2, W3, b3, out):
             if t - 2 < STEPS - SOON:
                 scale_late(t - 2)
             if t == 0:
-                regroup_pass(2, 0, "vector")
-                regroup_pass(2, 1, "vector")
                 regroup(3)
                 quantise(2)
             else:

@@ -53,6 +53,8 @@ def tile_gat_pa_t_kernel(tc, x, W1, b1, W2, b2, W3, b3, out):
 
         identity = const.tile([P, P], F32)
         make_identity(nc, identity[:])
+        identity_bf = const.tile([P, P], BF16)
+        nc.gpsimd.tensor_copy(out=identity_bf[:], in_=identity[:])
         bias_rows = const.tile([P, HEADS, DIM], BF16)
         nc.vector.memset(bias_rows[:], 0.0)
         ones = const.tile([P, P], BF16)
@@ -136,7 +138,7 @@ def tile_gat_pa_t_kernel(tc, x, W1, b1, W2, b2, W3, b3, out):
             {}, {}, {}, {}, {}, {}, {}, {}, {}, {},
         )
 
-        def regroup_pass(s, g, engine):
+        def regroup_pass(s, g):
             if not 0 <= s < STEPS:
                 return
             group, part = divmod(s, STEPS_PER_GROUP)
@@ -148,14 +150,35 @@ def tile_gat_pa_t_kernel(tc, x, W1, b1, W2, b2, W3, b3, out):
             source = x_raw[c][:, g, :, first : first + GROUP].rearrange("p j (m r) -> p m j r", r=SIDE)[
                 :, :, :, part * PAIR : (part + 1) * PAIR
             ]
-            if engine == "vector":
-                nc.vector.tensor_copy(out=target, in_=source)
-            else:
-                nc.scalar.copy(out=target, in_=source)
+            nc.vector.tensor_copy(out=target, in_=source)
+
+        interleaved = {}
+
+        def interleave(s):
+            if not 0 <= s < STEPS:
+                return
+            group, part = divmod(s, STEPS_PER_GROUP)
+            c, first = home[group]
+            words = psum_prep.tile([P, STEP, PACK], BF16, tag="prep")
+            for i in range(PAIR):
+                source = x_raw[c][:, 1, :, first : first + GROUP].rearrange("p j (m r) -> p m j r", r=SIDE)
+                nc.tensor.matmul(
+                    out=words[:, i * P : (i + 1) * P, :].rearrange("p m j -> p (m j)"),
+                    lhsT=identity_bf[:],
+                    rhs=source[:, :, :, part * PAIR + i],
+                    start=True,
+                    stop=True,
+                )
+            interleaved[s] = words
+
+        def collect(s):
+            if not 0 <= s < STEPS:
+                return
+            nc.scalar.copy(out=grouped[s][:, 1], in_=interleaved[s][:])
 
         def regroup(s):
-            regroup_pass(s, 0, "vector")
-            regroup_pass(s, 1, "scalar")
+            regroup_pass(s, 0)
+            collect(s)
 
         def quantise(s):
             if not 0 <= s < STEPS:
@@ -274,7 +297,7 @@ def tile_gat_pa_t_kernel(tc, x, W1, b1, W2, b2, W3, b3, out):
                 return
             for k in range(HEADS):
                 if second_engine(s) == "gpsimd":
-                    scale(s, k, 0, "scalar" if k == 0 and s % 2 == 0 else "vector")
+                    scale(s, k, 0, "scalar" if k < 2 else "vector")
                 else:
                     scale(s, k, 0, "vector")
                     scale(s, k, 1, "scalar" if k >= STEPS - s else "vector")
@@ -283,21 +306,25 @@ def tile_gat_pa_t_kernel(tc, x, W1, b1, W2, b2, W3, b3, out):
         prepare_weights(0, 0)
         prepare_weights(0, 1)
         spread_biases()
-        regroup_pass(0, 0, "vector")
-        regroup_pass(1, 0, "vector")
+        regroup_pass(0, 0)
+        regroup_pass(1, 0)
         prepare_weights(1, 0)
         prepare_weights(1, 1)
-        regroup_pass(0, 1, "vector")
+        interleave(0)
+        collect(0)
         prepare_weights(2, 0)
-        regroup_pass(1, 1, "scalar")
+        interleave(1)
+        collect(1)
         quantise(0)
         turn_weights(2, 1)
         quantise(1)
         quantise_weights(2, 1)
+        interleave(2)
         multiply(0)
-        regroup_pass(2, 0, "vector")
-        regroup_pass(2, 1, "scalar")
+        regroup_pass(2, 0)
+        collect(2)
         for t in range(STEPS + 1):
+            interleave(t + 3)
             multiply(t + 1)
             add_bias(t)
             sum_squares(t)

@@ -146,10 +146,9 @@ def tile_gat_pa_t_kernel(tc, x, W1, b1, W2, b2, W3, b3, out):
             if g == 0:
                 side_by_side = stage.tile([P, PASSES, STEP, PACK], BF16, align_bytes=64)
                 grouped[s] = side_by_side
-            target = grouped[s][:, g].rearrange("p (i m) j -> p m j i", i=PAIR)
-            source = x_raw[c][:, g, :, first : first + GROUP].rearrange("p j (m r) -> p m j r", r=SIDE)[
-                :, :, :, part * PAIR : (part + 1) * PAIR
-            ]
+            target = grouped[s][:, g].rearrange("p (c i) j -> p c j i", i=SIDE)
+            first += part * STEP
+            source = x_raw[c][:, g, :, first : first + STEP].rearrange("p j (c i) -> p c j i", i=SIDE)
             nc.vector.tensor_copy(out=target, in_=source)
 
         interleaved = {}
@@ -161,11 +160,11 @@ def tile_gat_pa_t_kernel(tc, x, W1, b1, W2, b2, W3, b3, out):
             c, first = home[group]
             words = psum_prep.tile([P, STEP, PACK], BF16, tag="prep")
             for i in range(PAIR):
-                source = x_raw[c][:, 1, :, first : first + GROUP].rearrange("p j (m r) -> p m j r", r=SIDE)
+                node = first + part * STEP + i * P
                 nc.tensor.matmul(
-                    out=words[:, i * P : (i + 1) * P, :].rearrange("p m j -> p (m j)"),
+                    out=words[:, i * P : (i + 1) * P, :].rearrange("p m j -> p j m"),
                     lhsT=identity_bf[:],
-                    rhs=source[:, :, :, part * PAIR + i],
+                    rhs=x_raw[c][:, 1, :, node : node + P],
                     start=True,
                     stop=True,
                 )
@@ -274,11 +273,8 @@ def tile_gat_pa_t_kernel(tc, x, W1, b1, W2, b2, W3, b3, out):
                 )
 
         def store(s, k):
-            group, part = divmod(s, STEPS_PER_GROUP)
             nc.sync.dma_start(
-                out=out[k, group * GROUP : (group + 1) * GROUP, :].rearrange("(m r) d -> m r d", r=SIDE)[
-                    :, part * PAIR : (part + 1) * PAIR, :
-                ],
+                out=out[k, s * STEP : (s + 1) * STEP, :].rearrange("(i m) d -> m i d", i=PAIR),
                 in_=result[s][:, k],
             )
 

@@ -21,15 +21,16 @@ HEADS = 3
 DIM = 256
 EPS = 1e-12
 
-GROUP = 512
-SIDE = GROUP // P
-CHUNK_GROUPS = (1, 1, 2, 2, 2)
+CHUNKS = (512, 512, 512, 512, 1024, 1024)
 PAIR = 2
 STEP = PAIR * P
 STEPS = NODES // STEP
-STEPS_PER_GROUP = GROUP // STEP
+RUN = 4
 
+AHEAD = 4
 SOON = 3
+
+DRAINED = STEPS - AHEAD - 1
 
 FLOPS = 2 * NODES * FEATURES * HEADS * DIM
 
@@ -41,13 +42,13 @@ def tile_gat_pa_t_kernel(tc, x, W1, b1, W2, b2, W3, b3, out):
     with ExitStack() as stack:
         const = stack.enter_context(tc.tile_pool(name="const", bufs=1))
         prep = stack.enter_context(tc.tile_pool(name="prep", bufs=3))
-        stage = stack.enter_context(tc.tile_pool(name="stage", bufs=4))
-        quantised = stack.enter_context(tc.tile_pool(name="quantised", bufs=4))
+        stage = stack.enter_context(tc.tile_pool(name="stage", bufs=5))
+        quantised = stack.enter_context(tc.tile_pool(name="quantised", bufs=6))
         biased = stack.enter_context(tc.tile_pool(name="biased", bufs=5))
         scratch = stack.enter_context(tc.tile_pool(name="scratch", bufs=2))
         results = stack.enter_context(tc.tile_pool(name="results", bufs=5))
         small = stack.enter_context(tc.tile_pool(name="small", bufs=5))
-        psum_prep = stack.enter_context(tc.psum_pool(name="psum_prep", bufs=2))
+        psum_words = stack.enter_context(tc.psum_pool(name="psum_words", bufs=2))
         psum = stack.enter_context(tc.psum_pool(name="psum", bufs=2 * HEADS))
         stack.enter_context(tc.manual_schedule())
 
@@ -67,18 +68,17 @@ def tile_gat_pa_t_kernel(tc, x, W1, b1, W2, b2, W3, b3, out):
         x_raw = []
         first_node = []
         home = {}
-        for c, groups in enumerate(CHUNK_GROUPS):
-            raw = const.tile([P, PASSES, PACK, groups * GROUP], BF16, name="x_raw%d" % c)
+        for c, count in enumerate(CHUNKS):
+            raw = const.tile([P, PASSES, PACK, count], BF16, name="x_raw%d" % c)
             x_raw.append(raw)
-            first_node.append(len(home) * GROUP)
-            for part in range(groups):
-                home[len(home)] = (c, part * GROUP)
+            first_node.append(len(home) * STEP)
+            for part in range(count // STEP):
+                home[len(home)] = (c, part * STEP)
 
         def load_nodes(c, g):
-            count = CHUNK_GROUPS[c] * GROUP
             nc.sync.dma_start(
                 out=x_raw[c][:, g, :, :],
-                in_=x_rows[g * K_PASS : (g + 1) * K_PASS, first_node[c] : first_node[c] + count].rearrange(
+                in_=x_rows[g * K_PASS : (g + 1) * K_PASS, first_node[c] : first_node[c] + CHUNKS[c]].rearrange(
                     "(p j) n -> p j n", j=PACK
                 ),
             )
@@ -86,16 +86,26 @@ def tile_gat_pa_t_kernel(tc, x, W1, b1, W2, b2, W3, b3, out):
         def load_weights(k, w):
             nc.sync.dma_start(out=w_rows[:, k], in_=w.rearrange("(half p) f -> p half f", p=P))
 
+        def load_biases():
+            for k, b in enumerate((b1, b2, b3)):
+                nc.sync.dma_start(out=bias_rows[0:1, k, :], in_=b.rearrange("(o d) -> o d", o=1))
+
+        load_nodes(0, 0)
+        load_biases()
+        load_nodes(0, 1)
         load_weights(0, W1)
         load_weights(1, W2)
-        for k, b in enumerate((b1, b2, b3)):
-            nc.sync.dma_start(out=bias_rows[0:1, k, :], in_=b.rearrange("(o d) -> o d", o=1))
-        load_nodes(0, 0)
         load_weights(2, W3)
-        load_nodes(0, 1)
-        for c in range(1, len(CHUNK_GROUPS)):
-            for g in range(PASSES):
-                load_nodes(c, g)
+        load_nodes(1, 0)
+        load_nodes(1, 1)
+        load_nodes(2, 0)
+        load_nodes(2, 1)
+        load_nodes(3, 0)
+        load_nodes(3, 1)
+        load_nodes(4, 0)
+        load_nodes(4, 1)
+        load_nodes(5, 0)
+        load_nodes(5, 1)
 
         bias_all = const.tile([P, HEADS, DIM], F32)
         w_codes = const.tile([P, PASSES, HEADS, DIM], U32, align_bytes=64)
@@ -104,7 +114,7 @@ def tile_gat_pa_t_kernel(tc, x, W1, b1, W2, b2, W3, b3, out):
         turned = {}
 
         def turn_weights(k, g):
-            flipped = psum_prep.tile([P, 2, DIM], F32, tag="prep")
+            flipped = psum.tile([P, 2, DIM], F32, tag="bank")
             for half in range(DIM // P):
                 words = w_rows[:, k, half, :].bitcast(F32).rearrange("d (g p u) -> d g u p", g=PASSES, u=2)
                 for u in range(2):
@@ -124,43 +134,23 @@ def tile_gat_pa_t_kernel(tc, x, W1, b1, W2, b2, W3, b3, out):
                 in_=turned[k, g][:].rearrange("p d u -> p (d u)").bitcast(BF16),
             )
 
-        def prepare_weights(k, g):
-            turn_weights(k, g)
-            quantise_weights(k, g)
-
         def spread_biases():
             for k in range(HEADS):
-                spread = psum_prep.tile([P, DIM], F32, tag="prep")
+                spread = psum_words.tile([P, DIM], F32, tag="words")
                 nc.tensor.matmul(out=spread[:], lhsT=ones[:], rhs=bias_rows[:, k, :], start=True, stop=True)
                 nc.scalar.copy(out=bias_all[:, k, :], in_=spread[:])
 
-        grouped, x_codes, x_scales, sums, biased_rows, sumsq, norm, floored, inv_norm, result = (
+        grouped, interleaved, x_codes, x_scales, sums, biased_rows, sumsq, norm, inv_norm, result = (
             {}, {}, {}, {}, {}, {}, {}, {}, {}, {},
         )
-
-        def regroup_pass(s, g):
-            if not 0 <= s < STEPS:
-                return
-            group, part = divmod(s, STEPS_PER_GROUP)
-            c, first = home[group]
-            if g == 0:
-                side_by_side = stage.tile([P, PASSES, STEP, PACK], BF16, align_bytes=64)
-                grouped[s] = side_by_side
-            target = grouped[s][:, g].rearrange("p (c i) j -> p c j i", i=SIDE)
-            first += part * STEP
-            source = x_raw[c][:, g, :, first : first + STEP].rearrange("p j (c i) -> p c j i", i=SIDE)
-            nc.vector.tensor_copy(out=target, in_=source)
-
-        interleaved = {}
 
         def interleave(s):
             if not 0 <= s < STEPS:
                 return
-            group, part = divmod(s, STEPS_PER_GROUP)
-            c, first = home[group]
-            words = psum_prep.tile([P, STEP, PACK], BF16, tag="prep")
+            c, first = home[s]
+            words = psum_words.tile([P, STEP, PACK], BF16, tag="words")
             for i in range(PAIR):
-                node = first + part * STEP + i * P
+                node = first + i * P
                 nc.tensor.matmul(
                     out=words[:, i * P : (i + 1) * P, :].rearrange("p m j -> p j m"),
                     lhsT=identity_bf[:],
@@ -170,14 +160,29 @@ def tile_gat_pa_t_kernel(tc, x, W1, b1, W2, b2, W3, b3, out):
                 )
             interleaved[s] = words
 
+        def open_stage(s):
+            side_by_side = stage.tile([P, PASSES, STEP, PACK], BF16, align_bytes=64)
+            grouped[s] = side_by_side
+
         def collect(s):
             if not 0 <= s < STEPS:
                 return
+            if s not in grouped:
+                open_stage(s)
             nc.scalar.copy(out=grouped[s][:, 1], in_=interleaved[s][:])
 
+        def regroup_pass(s, g, copy):
+            if s not in grouped:
+                open_stage(s)
+            c, first = home[s]
+            copy(
+                out=grouped[s][:, g].rearrange("p (c i) j -> p c j i", i=RUN),
+                in_=x_raw[c][:, g, :, first : first + STEP].rearrange("p j (c i) -> p c j i", i=RUN),
+            )
+
         def regroup(s):
-            regroup_pass(s, 0)
-            collect(s)
+            if 0 <= s < STEPS:
+                regroup_pass(s, 0, nc.vector.tensor_copy)
 
         def quantise(s):
             if not 0 <= s < STEPS:
@@ -191,52 +196,63 @@ def tile_gat_pa_t_kernel(tc, x, W1, b1, W2, b2, W3, b3, out):
             )
             x_codes[s], x_scales[s] = codes, scales
 
-        def multiply(s):
+        def multiply_head(s, k):
             if not 0 <= s < STEPS:
                 return
+            acc = psum.tile([P, PAIR, DIM], F32, tag="bank")
+            for i in range(PAIR):
+                nodes = slice(i * P, (i + 1) * P)
+                for g in range(PASSES):
+                    nc.tensor.matmul_mx(
+                        out=acc[:, i, :],
+                        lhsT=x_codes[s][:, g, nodes].bitcast(FP8X4),
+                        lhsT_scale=x_scales[s][:, g, nodes],
+                        rhs=w_codes[:, g, k, :].bitcast(FP8X4),
+                        rhs_scale=w_scales[:, g, k, :],
+                        start=(g == 0),
+                        stop=(g == PASSES - 1),
+                    )
+            sums[s, k] = acc
+
+        def multiply(s):
             for k in range(HEADS):
-                acc = psum.tile([P, PAIR, DIM], F32)
-                for i in range(PAIR):
-                    nodes = slice(i * P, (i + 1) * P)
-                    for g in range(PASSES):
-                        nc.tensor.matmul_mx(
-                            out=acc[:, i, :],
-                            lhsT=x_codes[s][:, g, nodes].bitcast(FP8X4),
-                            lhsT_scale=x_scales[s][:, g, nodes],
-                            rhs=w_codes[:, g, k, :].bitcast(FP8X4),
-                            rhs_scale=w_scales[:, g, k, :],
-                            start=(g == 0),
-                            stop=(g == PASSES - 1),
-                        )
-                sums[s, k] = acc
+                multiply_head(s, k)
+
+        def add_bias_head(s, k):
+            if not 0 <= s < STEPS:
+                return
+            if s not in biased_rows:
+                h = biased.tile([P, HEADS, PAIR, DIM], F32)
+                biased_rows[s] = h
+            nc.vector.tensor_tensor(
+                out=biased_rows[s][:, k],
+                in0=sums[s, k][:],
+                in1=bias_all[:, k, :].unsqueeze(1).to_broadcast([P, PAIR, DIM]),
+                op=ALU.add,
+            )
+
+        def sum_squares_head(s, k):
+            if not 0 <= s < STEPS:
+                return
+            if s not in sumsq:
+                total = small.tile([P, HEADS, PAIR], F32)
+                sumsq[s] = total
+            squares = scratch.tile([P, PAIR, DIM], F32)
+            for i in range(PAIR):
+                nc.scalar.activation(
+                    out=squares[:, i, :],
+                    in_=biased_rows[s][:, k, i, :],
+                    func=ACT.Square,
+                    accum_out=sumsq[s][:, k, i : i + 1],
+                )
 
         def add_bias(s):
-            if not 0 <= s < STEPS:
-                return
-            h = biased.tile([P, HEADS, PAIR, DIM], F32)
             for k in range(HEADS):
-                nc.vector.tensor_tensor(
-                    out=h[:, k],
-                    in0=sums[s, k][:],
-                    in1=bias_all[:, k, :].unsqueeze(1).to_broadcast([P, PAIR, DIM]),
-                    op=ALU.add,
-                )
-            biased_rows[s] = h
+                add_bias_head(s, k)
 
         def sum_squares(s):
-            if not 0 <= s < STEPS:
-                return
-            squares = scratch.tile([P, HEADS, PAIR, DIM], F32)
-            total = small.tile([P, HEADS, PAIR], F32)
             for k in range(HEADS):
-                for i in range(PAIR):
-                    nc.scalar.activation(
-                        out=squares[:, k, i, :],
-                        in_=biased_rows[s][:, k, i, :],
-                        func=ACT.Square,
-                        accum_out=total[:, k, i : i + 1],
-                    )
-            sumsq[s] = total
+                sum_squares_head(s, k)
 
         def take_root(s):
             if not 0 <= s < STEPS:
@@ -244,11 +260,6 @@ def tile_gat_pa_t_kernel(tc, x, W1, b1, W2, b2, W3, b3, out):
             root = small.tile([P, HEADS, PAIR], F32)
             nc.scalar.activation(out=root[:], in_=sumsq[s][:], func=ACT.Abs_reciprocal_sqrt)
             norm[s] = root
-
-        def floor_norm(s):
-            if not 0 <= s < STEPS:
-                return
-            return
 
         def invert(s):
             if not 0 <= s < STEPS:
@@ -293,50 +304,74 @@ def tile_gat_pa_t_kernel(tc, x, W1, b1, W2, b2, W3, b3, out):
                 return
             for k in range(HEADS):
                 if second_engine(s) == "gpsimd":
-                    scale(s, k, 0, "scalar" if k < 2 else "vector")
+                    scale(s, k, 0, "scalar" if k < 2 and s < DRAINED else "vector")
                 else:
                     scale(s, k, 0, "vector")
                     scale(s, k, 1, "scalar" if k >= STEPS - s else "vector")
                 store(s, k)
 
-        prepare_weights(0, 0)
-        prepare_weights(0, 1)
         spread_biases()
-        regroup_pass(0, 0)
-        regroup_pass(1, 0)
-        prepare_weights(1, 0)
-        prepare_weights(1, 1)
-        interleave(0)
-        collect(0)
-        prepare_weights(2, 0)
-        interleave(1)
-        collect(1)
+        regroup(0)
+        regroup_pass(0, 1, nc.scalar.copy)
+        regroup(1)
         quantise(0)
-        turn_weights(2, 1)
+        regroup_pass(1, 1, nc.scalar.copy)
+        turn_weights(0, 0)
+        turn_weights(0, 1)
         quantise(1)
+        quantise_weights(0, 0)
+        quantise_weights(0, 1)
+        turn_weights(1, 0)
+        turn_weights(1, 1)
+        multiply_head(0, 0)
+        multiply_head(1, 0)
+        quantise_weights(1, 0)
+        quantise_weights(1, 1)
+        regroup_pass(2, 1, nc.scalar.copy)
+        turn_weights(2, 0)
+        turn_weights(2, 1)
+        regroup(2)
+        add_bias_head(0, 0)
+        sum_squares_head(0, 0)
+        multiply_head(0, 1)
+        add_bias_head(1, 0)
+        sum_squares_head(1, 0)
+        regroup(3)
+        quantise_weights(2, 0)
         quantise_weights(2, 1)
-        interleave(2)
-        multiply(0)
-        regroup_pass(2, 0)
-        collect(2)
+        multiply_head(1, 1)
+        regroup_pass(3, 1, nc.scalar.copy)
+        add_bias_head(0, 1)
+        sum_squares_head(0, 1)
+        multiply_head(0, 2)
+        quantise(2)
+        add_bias_head(1, 1)
+        sum_squares_head(1, 1)
+        multiply_head(1, 2)
+        add_bias_head(0, 2)
+        sum_squares_head(0, 2)
+        take_root(0)
+        regroup(4)
         for t in range(STEPS + 1):
-            interleave(t + 3)
-            multiply(t + 1)
-            add_bias(t)
-            sum_squares(t)
+            if t > 0:
+                multiply(t + 1)
+                if t == 1:
+                    add_bias_head(1, 2)
+                    sum_squares_head(1, 2)
+                else:
+                    add_bias(t)
+                    sum_squares(t)
+            interleave(t + AHEAD)
             if t - 2 < STEPS - SOON:
                 scale_late(t - 2)
-            if t == 0:
-                regroup(3)
-                quantise(2)
-            else:
-                quantise(t + 2)
+            quantise(t + AHEAD - 1)
             invert(t - 1)
             scale_early(t - 1)
             if t - 1 >= STEPS - SOON:
                 take_root(t)
                 scale_late(t - 1)
             else:
+                regroup(t + AHEAD + 1)
+                collect(t + AHEAD)
                 if t > 0:
-                    regroup(t + 3)
-                take_root(t)
+                    take_root(t)

@@ -21,7 +21,7 @@ HEADS = 3
 DIM = 256
 EPS = 1e-12
 
-CHUNKS = (512, 512, 512, 512, 1024, 1024)
+CHUNKS = (512, 512, 1024, 1024, 1024)
 PAIR = 2
 STEP = PAIR * P
 STEPS = NODES // STEP
@@ -31,7 +31,7 @@ AHEAD = 4
 SOON = 3
 
 DRAINED = STEPS - AHEAD - 1
-
+LAST = (("vector", "vector"), ("vector", "vector"), ("vector", "scalar"))
 FLOPS = 2 * NODES * FEATURES * HEADS * DIM
 
 
@@ -104,8 +104,6 @@ def tile_gat_pa_t_kernel(tc, x, W1, b1, W2, b2, W3, b3, out):
         load_nodes(3, 1)
         load_nodes(4, 0)
         load_nodes(4, 1)
-        load_nodes(5, 0)
-        load_nodes(5, 1)
 
         bias_all = const.tile([P, HEADS, DIM], F32)
         w_codes = const.tile([P, PASSES, HEADS, DIM], U32, align_bytes=64)
@@ -149,12 +147,12 @@ def tile_gat_pa_t_kernel(tc, x, W1, b1, W2, b2, W3, b3, out):
                 return
             c, first = home[s]
             words = psum_words.tile([P, STEP, PACK], BF16, tag="words")
-            for i in range(PAIR):
-                node = first + i * P
+            places = words[:].rearrange("p (i m) j -> p j m i", i=PAIR)
+            for j in range(0, PACK, 2):
                 nc.tensor.matmul(
-                    out=words[:, i * P : (i + 1) * P, :].rearrange("p m j -> p j m"),
+                    out=places[:, j : j + 2],
                     lhsT=identity_bf[:],
-                    rhs=x_raw[c][:, 1, :, node : node + P],
+                    rhs=x_raw[c][:, 1, j : j + 2, first : first + STEP],
                     start=True,
                     stop=True,
                 )
@@ -176,8 +174,8 @@ def tile_gat_pa_t_kernel(tc, x, W1, b1, W2, b2, W3, b3, out):
                 open_stage(s)
             c, first = home[s]
             copy(
-                out=grouped[s][:, g].rearrange("p (c i) j -> p c j i", i=RUN),
-                in_=x_raw[c][:, g, :, first : first + STEP].rearrange("p j (c i) -> p c j i", i=RUN),
+                out=grouped[s][:, g].rearrange("p (i c r) j -> p c j r i", i=PAIR, r=RUN // PAIR),
+                in_=x_raw[c][:, g, :, first : first + STEP].rearrange("p j (c r i) -> p c j r i", i=PAIR, r=RUN // PAIR),
             )
 
         def regroup(s):
@@ -254,6 +252,18 @@ def tile_gat_pa_t_kernel(tc, x, W1, b1, W2, b2, W3, b3, out):
             for k in range(HEADS):
                 sum_squares_head(s, k)
 
+        def finish_head(s, k, engines):
+            if s not in result:
+                scaled = results.tile([P, HEADS, PAIR, DIM], F32)
+                result[s] = scaled
+            root = small.tile([P, PAIR], F32)
+            nc.scalar.activation(out=root[:], in_=sumsq[s][:, k, :], func=ACT.Abs_reciprocal_sqrt)
+            inverse = small.tile([P, PAIR], F32)
+            nc.vector.tensor_scalar_min(out=inverse[:], in0=root[:], scalar1=1.0 / EPS)
+            for i in range(PAIR):
+                scale_by(s, k, i, inverse[:, i : i + 1], engines[i])
+            store(s, k)
+
         def take_root(s):
             if not 0 <= s < STEPS:
                 return
@@ -271,9 +281,11 @@ def tile_gat_pa_t_kernel(tc, x, W1, b1, W2, b2, W3, b3, out):
             result[s] = scaled
 
         def scale(s, k, i, engine):
+            scale_by(s, k, i, inv_norm[s][:, k, i : i + 1], engine)
+
+        def scale_by(s, k, i, factor, engine):
             target = result[s][:, k, i, :]
             rows = biased_rows[s][:, k, i, :]
-            factor = inv_norm[s][:, k, i : i + 1]
             if engine == "vector":
                 nc.vector.tensor_scalar_mul(out=target, in0=rows, scalar1=factor)
             elif engine == "scalar":
@@ -285,7 +297,7 @@ def tile_gat_pa_t_kernel(tc, x, W1, b1, W2, b2, W3, b3, out):
 
         def store(s, k):
             nc.sync.dma_start(
-                out=out[k, s * STEP : (s + 1) * STEP, :].rearrange("(i m) d -> m i d", i=PAIR),
+                out=out[k, s * STEP : (s + 1) * STEP, :].rearrange("(m i) d -> m i d", i=PAIR),
                 in_=result[s][:, k],
             )
 
@@ -299,12 +311,15 @@ def tile_gat_pa_t_kernel(tc, x, W1, b1, W2, b2, W3, b3, out):
                 for k in range(HEADS):
                     scale(s, k, 1, "gpsimd")
 
-        def scale_late(s):
+        def scale_late(s, only=("vector", "scalar")):
             if not 0 <= s < STEPS:
                 return
             for k in range(HEADS):
                 if second_engine(s) == "gpsimd":
-                    scale(s, k, 0, "scalar" if k < 2 and s < DRAINED else "vector")
+                    who = "scalar" if k < 2 and s < DRAINED else "vector"
+                    if who not in only:
+                        continue
+                    scale(s, k, 0, who)
                 else:
                     scale(s, k, 0, "vector")
                     scale(s, k, 1, "scalar" if k >= STEPS - s else "vector")
@@ -352,18 +367,30 @@ def tile_gat_pa_t_kernel(tc, x, W1, b1, W2, b2, W3, b3, out):
         sum_squares_head(0, 2)
         take_root(0)
         regroup(4)
-        for t in range(STEPS + 1):
+        for t in range(STEPS):
+            if t - 2 < STEPS - SOON and t < STEPS - 1:
+                scale_late(t - 2, ("scalar",))
             if t > 0:
                 multiply(t + 1)
                 if t == 1:
                     add_bias_head(1, 2)
                     sum_squares_head(1, 2)
-                else:
+                elif t < STEPS - 1:
                     add_bias(t)
                     sum_squares(t)
             interleave(t + AHEAD)
+            if t == STEPS - 1:
+                add_bias_head(t, 0)
+                invert(t - 1)
+                add_bias_head(t, 1)
+                scale_late(t - 1)
+                add_bias_head(t, 2)
+                for k in range(HEADS):
+                    sum_squares_head(t, k)
+                    finish_head(t, k, LAST[k])
+                continue
             if t - 2 < STEPS - SOON:
-                scale_late(t - 2)
+                scale_late(t - 2, ("vector",))
             quantise(t + AHEAD - 1)
             invert(t - 1)
             scale_early(t - 1)

@@ -44,10 +44,10 @@ def tile_gat_pa_t_kernel(tc, x, W1, b1, W2, b2, W3, b3, out):
         prep = stack.enter_context(tc.tile_pool(name="prep", bufs=3))
         stage = stack.enter_context(tc.tile_pool(name="stage", bufs=5))
         quantised = stack.enter_context(tc.tile_pool(name="quantised", bufs=6))
-        biased = stack.enter_context(tc.tile_pool(name="biased", bufs=5))
+        biased = stack.enter_context(tc.tile_pool(name="biased", bufs=8))
         scratch = stack.enter_context(tc.tile_pool(name="scratch", bufs=2))
-        results = stack.enter_context(tc.tile_pool(name="results", bufs=5))
-        small = stack.enter_context(tc.tile_pool(name="small", bufs=5))
+        results = stack.enter_context(tc.tile_pool(name="results", bufs=8))
+        small = stack.enter_context(tc.tile_pool(name="small", bufs=24))
         psum_words = stack.enter_context(tc.psum_pool(name="psum_words", bufs=2))
         psum = stack.enter_context(tc.psum_pool(name="psum", bufs=2 * HEADS))
         stack.enter_context(tc.manual_schedule())

@@ -30,7 +30,7 @@ RUN = 4
 AHEAD = 4
 SOON = 3
 
-DRAINED = STEPS - AHEAD - 1
+DRAINED = STEPS - AHEAD + 1
 LAST = (("vector", "vector"), ("vector", "vector"), ("vector", "scalar"))
 FLOPS = 2 * NODES * FEATURES * HEADS * DIM
 
@@ -84,7 +84,7 @@ def tile_gat_pa_t_kernel(tc, x, W1, b1, W2, b2, W3, b3, out):
             )
 
         def load_weights(k, w):
-            nc.sync.dma_start(out=w_rows[:, k], in_=w.rearrange("(half p) f -> p half f", p=P))
+            nc.sync.dma_start(out=w_rows[:, k], in_=w.rearrange("(p half) f -> p half f", p=P))
 
         def load_biases():
             for k, b in enumerate((b1, b2, b3)):
@@ -122,7 +122,10 @@ def tile_gat_pa_t_kernel(tc, x, W1, b1, W2, b2, W3, b3, out):
                         identity=identity[:],
                     )
             w_grouped = prep.tile([P, DIM, 2], F32, align_bytes=64)
-            nc.scalar.copy(out=w_grouped[:], in_=flipped[:].rearrange("p u d -> p d u"))
+            nc.scalar.copy(
+                out=w_grouped[:].rearrange("p (q half) u -> p q half u", half=DIM // P),
+                in_=flipped[:].rearrange("p u (half q) -> p q half u", half=DIM // P),
+            )
             turned[k, g] = w_grouped
 
         def quantise_weights(k, g):
@@ -368,6 +371,7 @@ def tile_gat_pa_t_kernel(tc, x, W1, b1, W2, b2, W3, b3, out):
         take_root(0)
         regroup(4)
         for t in range(STEPS):
+            lead = AHEAD if t == 0 else AHEAD - 1
             if t - 2 < STEPS - SOON and t < STEPS - 1:
                 scale_late(t - 2, ("scalar",))
             if t > 0:
@@ -378,8 +382,11 @@ def tile_gat_pa_t_kernel(tc, x, W1, b1, W2, b2, W3, b3, out):
                 elif t < STEPS - 1:
                     add_bias(t)
                     sum_squares(t)
-            interleave(t + AHEAD)
+            if t != 1:
+                interleave(t + lead)
             if t == STEPS - 1:
+                if t - 2 < STEPS - SOON:
+                    scale_late(t - 2)
                 add_bias_head(t, 0)
                 invert(t - 1)
                 add_bias_head(t, 1)
@@ -391,14 +398,16 @@ def tile_gat_pa_t_kernel(tc, x, W1, b1, W2, b2, W3, b3, out):
                 continue
             if t - 2 < STEPS - SOON:
                 scale_late(t - 2, ("vector",))
-            quantise(t + AHEAD - 1)
+            if t != 1:
+                quantise(t + lead - 1)
             invert(t - 1)
             scale_early(t - 1)
             if t - 1 >= STEPS - SOON:
                 take_root(t)
                 scale_late(t - 1)
             else:
-                regroup(t + AHEAD + 1)
-                collect(t + AHEAD)
+                if t != 1:
+                    regroup(t + lead + 1)
+                    collect(t + lead)
                 if t > 0:
                     take_root(t)

@@ -30,7 +30,7 @@ RUN = 4
 AHEAD = 4
 SOON = 3
 
-DRAINED = STEPS - AHEAD + 1
+DRAINED = STEPS - AHEAD
 LAST = (("vector", "vector"), ("vector", "vector"), ("vector", "scalar"))
 FLOPS = 2 * NODES * FEATURES * HEADS * DIM
 
@@ -319,7 +319,7 @@ def tile_gat_pa_t_kernel(tc, x, W1, b1, W2, b2, W3, b3, out):
                 return
             for k in range(HEADS):
                 if second_engine(s) == "gpsimd":
-                    who = "scalar" if k < 2 and s < DRAINED else "vector"
+                    who = "scalar" if k < 1 + (s % 4 > 0) and s < DRAINED else "vector"
                     if who not in only:
                         continue
                     scale(s, k, 0, who)

from contextlib import ExitStack

import concourse.mybir as mybir
from concourse.masks import make_identity

F32 = mybir.dt.float32
BF16 = mybir.dt.bfloat16
U32 = mybir.dt.uint32
U8 = mybir.dt.uint8
FP8X4 = mybir.dt.float8_e4m3fn_x4
ACT = mybir.ActivationFunctionType
ALU = mybir.AluOpType

P = 128
PACK = 4
K_PASS = P * PACK
FEATURES = 1024
PASSES = FEATURES // K_PASS
NODES = 4096
HEADS = 3
DIM = 256
EPS = 1e-12

CHUNKS = (512, 512, 1024, 1024, 1024)
PAIR = 2
STEP = PAIR * P
STEPS = NODES // STEP
RUN = 4

AHEAD = 4
SOON = 3

DRAINED = STEPS - AHEAD
LAST = (("vector", "vector"), ("vector", "vector"), ("vector", "scalar"))
FLOPS = 2 * NODES * FEATURES * HEADS * DIM


def tile_gat_pa_t_kernel(tc, x, W1, b1, W2, b2, W3, b3, out):
    nc = tc.nc
    x_rows = x.rearrange("b f i j -> (b f) (i j)")

    with ExitStack() as stack:
        const = stack.enter_context(tc.tile_pool(name="const", bufs=1))
        prep = stack.enter_context(tc.tile_pool(name="prep", bufs=3))
        stage = stack.enter_context(tc.tile_pool(name="stage", bufs=5))
        quantised = stack.enter_context(tc.tile_pool(name="quantised", bufs=6))
        biased = stack.enter_context(tc.tile_pool(name="biased", bufs=8))
        scratch = stack.enter_context(tc.tile_pool(name="scratch", bufs=2))
        results = stack.enter_context(tc.tile_pool(name="results", bufs=8))
        small = stack.enter_context(tc.tile_pool(name="small", bufs=24))
        psum_words = stack.enter_context(tc.psum_pool(name="psum_words", bufs=2))
        psum = stack.enter_context(tc.psum_pool(name="psum", bufs=2 * HEADS))
        stack.enter_context(tc.manual_schedule())

        identity = const.tile([P, P], F32)
        make_identity(nc, identity[:])
        identity_bf = const.tile([P, P], BF16)
        nc.gpsimd.tensor_copy(out=identity_bf[:], in_=identity[:])
        bias_rows = const.tile([P, HEADS, DIM], BF16)
        nc.vector.memset(bias_rows[:], 0.0)
        ones = const.tile([P, P], BF16)
        nc.vector.memset(ones[:], 1.0)
        one = const.tile([P, 1], F32)
        nc.vector.memset(one[:], 1.0)
        nc.scalar.activation(out=one[:], in_=one[:], func=ACT.Abs_reciprocal_sqrt)

        w_rows = const.tile([P, HEADS, DIM // P, FEATURES], BF16)
        x_raw = []
        first_node = []
        home = {}
        for c, count in enumerate(CHUNKS):
            raw = const.tile([P, PASSES, PACK, count], BF16, name="x_raw%d" % c)
            x_raw.append(raw)
            first_node.append(len(home) * STEP)
            for part in range(count // STEP):
                home[len(home)] = (c, part * STEP)

        def load_nodes(c, g):
            nc.sync.dma_start(
                out=x_raw[c][:, g, :, :],
                in_=x_rows[g * K_PASS : (g + 1) * K_PASS, first_node[c] : first_node[c] + CHUNKS[c]].rearrange(
                    "(p j) n -> p j n", j=PACK
                ),
            )

        def load_weights(k, w):
            nc.sync.dma_start(out=w_rows[:, k], in_=w.rearrange("(p half) f -> p half f", p=P))

        def load_biases():
            for k, b in enumerate((b1, b2, b3)):
                nc.sync.dma_start(out=bias_rows[0:1, k, :], in_=b.rearrange("(o d) -> o d", o=1))

        load_nodes(0, 0)
        load_biases()
        load_nodes(0, 1)
        load_weights(0, W1)
        load_weights(1, W2)
        load_weights(2, W3)
        load_nodes(1, 0)
        load_nodes(1, 1)
        load_nodes(2, 0)
        load_nodes(2, 1)
        load_nodes(3, 0)
        load_nodes(3, 1)
        load_nodes(4, 0)
        load_nodes(4, 1)

        bias_all = const.tile([P, HEADS, DIM], F32)
        w_codes = const.tile([P, PASSES, HEADS, DIM], U32, align_bytes=64)
        w_scales = const.tile([P, PASSES, HEADS, DIM], U8, align_bytes=64)

        turned = {}

        def turn_weights(k, g):
            flipped = psum.tile([P, 2, DIM], F32, tag="bank")
            for half in range(DIM // P):
                words = w_rows[:, k, half, :].bitcast(F32).rearrange("d (g p u) -> d g u p", g=PASSES, u=2)
                for u in range(2):
                    nc.tensor.transpose(
                        out=flipped[:, u, half * P : (half + 1) * P],
                        in_=words[:, g, u, :],
                        identity=identity[:],
                    )
            w_grouped = prep.tile([P, DIM, 2], F32, align_bytes=64)
            nc.scalar.copy(
                out=w_grouped[:].rearrange("p (q half) u -> p q half u", half=DIM // P),
                in_=flipped[:].rearrange("p u (half q) -> p q half u", half=DIM // P),
            )
            turned[k, g] = w_grouped

        def quantise_weights(k, g):
            nc.vector.quantize_mx(
                out=w_codes[:, g, k, :].bitcast(FP8X4),
                scales=w_scales[:, g, k, :],
                in_=turned[k, g][:].rearrange("p d u -> p (d u)").bitcast(BF16),
            )

        def spread_biases():
            for k in range(HEADS):
                spread = psum_words.tile([P, DIM], F32, tag="words")
                nc.tensor.matmul(out=spread[:], lhsT=ones[:], rhs=bias_rows[:, k, :], start=True, stop=True)
                nc.scalar.copy(out=bias_all[:, k, :], in_=spread[:])

        grouped, interleaved, x_codes, x_scales, sums, biased_rows, sumsq, norm, inv_norm, result = (
            {}, {}, {}, {}, {}, {}, {}, {}, {}, {},
        )

        def interleave(s):
            if not 0 <= s < STEPS:
                return
            c, first = home[s]
            words = psum_words.tile([P, STEP, PACK], BF16, tag="words")
            places = words[:].rearrange("p (i m) j -> p j m i", i=PAIR)
            for j in range(0, PACK, 2):
                nc.tensor.matmul(
                    out=places[:, j : j + 2],
                    lhsT=identity_bf[:],
                    rhs=x_raw[c][:, 1, j : j + 2, first : first + STEP],
                    start=True,
                    stop=True,
                )
            interleaved[s] = words

        def open_stage(s):
            side_by_side = stage.tile([P, PASSES, STEP, PACK], BF16, align_bytes=64)
            grouped[s] = side_by_side

        def collect(s):
            if not 0 <= s < STEPS:
                return
            if s not in grouped:
                open_stage(s)
            nc.scalar.copy(out=grouped[s][:, 1], in_=interleaved[s][:])

        def regroup_pass(s, g, copy):
            if s not in grouped:
                open_stage(s)
            c, first = home[s]
            copy(
                out=grouped[s][:, g].rearrange("p (i c r) j -> p c j r i", i=PAIR, r=RUN // PAIR),
                in_=x_raw[c][:, g, :, first : first + STEP].rearrange("p j (c r i) -> p c j r i", i=PAIR, r=RUN // PAIR),
            )

        def regroup(s):
            if 0 <= s < STEPS:
                regroup_pass(s, 0, nc.vector.tensor_copy)

        def quantise(s):
            if not 0 <= s < STEPS:
                return
            codes = quantised.tile([P, PASSES, STEP], U32, align_bytes=64)
            scales = quantised.tile([P, PASSES, STEP], U8, align_bytes=64)
            nc.vector.quantize_mx(
                out=codes[:].rearrange("p g n -> p (g n)").bitcast(FP8X4),
                scales=scales[:].rearrange("p g n -> p (g n)"),
                in_=grouped[s][:].rearrange("p g n j -> p (g n j)"),
            )
            x_codes[s], x_scales[s] = codes, scales

        def multiply_head(s, k):
            if not 0 <= s < STEPS:
                return
            acc = psum.tile([P, PAIR, DIM], F32, tag="bank")
            for i in range(PAIR):
                nodes = slice(i * P, (i + 1) * P)
                for g in range(PASSES):
                    nc.tensor.matmul_mx(
                        out=acc[:, i, :],
                        lhsT=x_codes[s][:, g, nodes].bitcast(FP8X4),
                        lhsT_scale=x_scales[s][:, g, nodes],
                        rhs=w_codes[:, g, k, :].bitcast(FP8X4),
                        rhs_scale=w_scales[:, g, k, :],
                        start=(g == 0),
                        stop=(g == PASSES - 1),
                    )
            sums[s, k] = acc

        def multiply(s):
            for k in range(HEADS):
                multiply_head(s, k)

        def add_bias_head(s, k):
            if not 0 <= s < STEPS:
                return
            if s not in biased_rows:
                h = biased.tile([P, HEADS, PAIR, DIM], F32)
                biased_rows[s] = h
            nc.vector.tensor_tensor(
                out=biased_rows[s][:, k],
                in0=sums[s, k][:],
                in1=bias_all[:, k, :].unsqueeze(1).to_broadcast([P, PAIR, DIM]),
                op=ALU.add,
            )

        def sum_squares_head(s, k):
            if not 0 <= s < STEPS:
                return
            if s not in sumsq:
                total = small.tile([P, HEADS, PAIR], F32)
                sumsq[s] = total
            squares = scratch.tile([P, PAIR, DIM], F32)
            for i in range(PAIR):
                nc.scalar.activation(
                    out=squares[:, i, :],
                    in_=biased_rows[s][:, k, i, :],
                    func=ACT.Square,
                    accum_out=sumsq[s][:, k, i : i + 1],
                )

        def add_bias(s):
            for k in range(HEADS):
                add_bias_head(s, k)

        def sum_squares(s):
            for k in range(HEADS):
                sum_squares_head(s, k)

        def finish_head(s, k, engines):
            if s not in result:
                scaled = results.tile([P, HEADS, PAIR, DIM], F32)
                result[s] = scaled
            root = small.tile([P, PAIR], F32)
            nc.scalar.activation(out=root[:], in_=sumsq[s][:, k, :], func=ACT.Abs_reciprocal_sqrt)
            inverse = small.tile([P, PAIR], F32)
            nc.vector.tensor_scalar_min(out=inverse[:], in0=root[:], scalar1=1.0 / EPS)
            for i in range(PAIR):
                scale_by(s, k, i, inverse[:, i : i + 1], engines[i])
            store(s, k)

        def take_root(s):
            if not 0 <= s < STEPS:
                return
            root = small.tile([P, HEADS, PAIR], F32)
            nc.scalar.activation(out=root[:], in_=sumsq[s][:], func=ACT.Abs_reciprocal_sqrt)
            norm[s] = root

        def invert(s):
            if not 0 <= s < STEPS:
                return
            inverse = small.tile([P, HEADS, PAIR], F32)
            nc.vector.tensor_scalar_min(out=inverse[:], in0=norm[s][:], scalar1=1.0 / EPS)
            inv_norm[s] = inverse
            scaled = results.tile([P, HEADS, PAIR, DIM], F32)
            result[s] = scaled

        def scale(s, k, i, engine):
            scale_by(s, k, i, inv_norm[s][:, k, i : i + 1], engine)

        def scale_by(s, k, i, factor, engine):
            target = result[s][:, k, i, :]
            rows = biased_rows[s][:, k, i, :]
            if engine == "vector":
                nc.vector.tensor_scalar_mul(out=target, in0=rows, scalar1=factor)
            elif engine == "scalar":
                nc.scalar.activation(out=target, in_=rows, func=ACT.Copy, scale=factor)
            else:
                nc.gpsimd.tensor_scalar(
                    out=target, in0=rows, scalar1=factor, scalar2=0.0, op0=ALU.mult, op1=ALU.add
                )

        def store(s, k):
            nc.sync.dma_start(
                out=out[k, s * STEP : (s + 1) * STEP, :].rearrange("(m i) d -> m i d", i=PAIR),
                in_=result[s][:, k],
            )

        def second_engine(s):
            return "gpsimd" if s < STEPS - 2 else "scalar"

        def scale_early(s):
            if not 0 <= s < STEPS:
                return
            if second_engine(s) == "gpsimd":
                for k in range(HEADS):
                    scale(s, k, 1, "gpsimd")

        def scale_late(s, only=("vector", "scalar")):
            if not 0 <= s < STEPS:
                return
            for k in range(HEADS):
                if second_engine(s) == "gpsimd":
                    who = "scalar" if k < 1 + (s % 4 > 0) and s < DRAINED else "vector"
                    if who not in only:
                        continue
                    scale(s, k, 0, who)
                else:
                    scale(s, k, 0, "vector")
                    scale(s, k, 1, "scalar" if k >= STEPS - s else "vector")
                store(s, k)

        spread_biases()
        regroup(0)
        regroup_pass(0, 1, nc.scalar.copy)
        regroup(1)
        quantise(0)
        regroup_pass(1, 1, nc.scalar.copy)
        turn_weights(0, 0)
        turn_weights(0, 1)
        quantise(1)
        quantise_weights(0, 0)
        quantise_weights(0, 1)
        turn_weights(1, 0)
        turn_weights(1, 1)
        multiply_head(0, 0)
        multiply_head(1, 0)
        quantise_weights(1, 0)
        quantise_weights(1, 1)
        regroup_pass(2, 1, nc.scalar.copy)
        turn_weights(2, 0)
        turn_weights(2, 1)
        regroup(2)
        add_bias_head(0, 0)
        sum_squares_head(0, 0)
        multiply_head(0, 1)
        add_bias_head(1, 0)
        sum_squares_head(1, 0)
        regroup(3)
        quantise_weights(2, 0)
        quantise_weights(2, 1)
        multiply_head(1, 1)
        regroup_pass(3, 1, nc.scalar.copy)
        add_bias_head(0, 1)
        sum_squares_head(0, 1)
        multiply_head(0, 2)
        quantise(2)
        add_bias_head(1, 1)
        sum_squares_head(1, 1)
        multiply_head(1, 2)
        add_bias_head(0, 2)
        sum_squares_head(0, 2)
        take_root(0)
        regroup(4)
        for t in range(STEPS):
            lead = AHEAD if t == 0 else AHEAD - 1
            if t - 2 < STEPS - SOON and t < STEPS - 1:
                scale_late(t - 2, ("scalar",))
            if t > 0:
                multiply(t + 1)
                if t == 1:
                    add_bias_head(1, 2)
                    sum_squares_head(1, 2)
                elif t < STEPS - 1:
                    add_bias(t)
                    sum_squares(t)
            if t != 1:
                interleave(t + lead)
            if t == STEPS - 1:
                if t - 2 < STEPS - SOON:
                    scale_late(t - 2)
                add_bias_head(t, 0)
                invert(t - 1)
                add_bias_head(t, 1)
                scale_late(t - 1)
                add_bias_head(t, 2)
                for k in range(HEADS):
                    sum_squares_head(t, k)
                    finish_head(t, k, LAST[k])
                continue
            if t - 2 < STEPS - SOON:
                scale_late(t - 2, ("vector",))
            if t != 1:
                quantise(t + lead - 1)
            invert(t - 1)
            scale_early(t - 1)
            if t - 1 >= STEPS - SOON:
                take_root(t)
                scale_late(t - 1)
            else:
                if t != 1:
                    regroup(t + lead + 1)
                    collect(t + lead)
                if t > 0:
                    take_root(t)
